import numpy as np
import ml_dtypes


def mxq(x, axis, fmt="e4m3"):
    dtype, down = {"e4m3": (ml_dtypes.float8_e4m3fn, 7), "e5m2": (ml_dtypes.float8_e5m2, 14)}[fmt]
    v = np.moveaxis(np.asarray(x, np.float32).astype(ml_dtypes.bfloat16).astype(np.float64), axis, -1)
    blocks = v.reshape(v.shape[:-1] + (-1, 32))
    amax = np.abs(blocks).max(-1, keepdims=True)
    byte = np.maximum(np.where(amax > 0, np.frexp(amax)[1] - 1 + 127, 0) - down, 1)
    scale = np.exp2(byte - 127.0)
    codes = (blocks / scale).astype(np.float32).astype(dtype).astype(np.float64)
    return np.moveaxis((codes * scale).reshape(v.shape), -1, axis)


WIDE = False


def mx_kscale(k):
    if not WIDE:
        return np.ones(k)
    levels = np.array([10, -10, 5, -5, 0])
    a = np.random.permutation(np.resize(levels, k // 512 * 4)).reshape(k // 512, 4)
    idx = np.arange(k)
    return np.exp2(a[idx // 512, idx % 128 // 32])


BF16 = ml_dtypes.bfloat16


def bf(x):
    return np.asarray(x, np.float32).astype(BF16)


def f64(x):
    return np.asarray(x).astype(np.float64)


B, N, K, H, C_E, M = 2, 128, 32, 512, 512, 512


def gelu_tanh(v):
    return 0.5 * v * (1.0 + np.tanh(np.sqrt(2.0 / np.pi) * (v + 0.044715 * v**3)))


def setup_inputs():
    sv, se = mx_kscale(H), mx_kscale(C_E)
    s = np.concatenate([sv, se])
    return {"h_V": bf(np.random.standard_normal((B, N, H)) * sv),
            "h_E": bf(np.random.standard_normal((B, N, K, C_E)) * se),
            "W1_w": bf(np.random.standard_normal((H + C_E, M)) / np.sqrt(H + C_E) / s[:, None]),
            "W1_b": bf(np.random.standard_normal(M) * 0.1),
            "W2_w": bf(np.random.standard_normal((M, M)) * 1.5 / np.sqrt(M)),
            "W2_b": bf(np.random.standard_normal(M) * 0.1)}


def reference(h_V, h_E, W1_w, W1_b, W2_w, W2_b):
    w1 = f64(W1_w)
    pv = mxq(f64(h_V), 2, "e4m3") @ mxq(w1[:H], 0, "e4m3")
    pe = mxq(f64(h_E), 3, "e4m3") @ mxq(w1[H:], 0, "e4m3")
    h1 = gelu_tanh(pv[:, :, None, :] + pe + f64(W1_b))
    return gelu_tanh((mxq(h1, 3, "e4m3") @ mxq(f64(W2_w), 0, "e4m3")) + f64(W2_b))

@@ -1,0 +1,276 @@
+from contextlib import ExitStack
+
+import concourse.mybir as mybir
+from concourse.masks import make_identity
+
+BF16 = mybir.dt.bfloat16
+F32 = mybir.dt.float32
+I32 = mybir.dt.int32
+U32 = mybir.dt.uint32
+U8 = mybir.dt.uint8
+FP8X4 = mybir.dt.float8_e4m3fn_x4
+GELU = mybir.ActivationFunctionType.Gelu_apprx_tanh
+ADD = mybir.AluOpType.add
+
+P = 128
+PACK = 4
+FEAT = P * PACK
+NODES = 256
+EDGES = 32
+ROWS = NODES * EDGES
+UNIT = 512
+SUBS = UNIT // P
+UNITS = ROWS // UNIT
+BLOCK_UNITS = 4
+BLOCKS = UNITS // BLOCK_UNITS
+BLOCK_NODES = NODES // BLOCKS
+COPIES = P // BLOCK_NODES
+
+FLOPS = 2 * FEAT * FEAT * (NODES + 2 * ROWS)
+
+
+def tile_declayerj_pa_t_kernel(tc, h_V, h_E, W1_w, W1_b, W2_w, W2_b, out):
+    nc = tc.nc
+
+    edge_units = h_E.rearrange("b n k c -> (b n k) c").rearrange(
+        "(g p j a) c -> g j p (a c)", p=P, j=BLOCK_UNITS, a=SUBS
+    )
+    out_units = out.rearrange("b n k c -> (b n k) c").rearrange(
+        "(g p j a) c -> g j p (a c)", p=P, j=BLOCK_UNITS, a=SUBS
+    )
+
+    with ExitStack() as ctx:
+        consts = ctx.enter_context(tc.tile_pool(name="consts", bufs=1))
+        prep = ctx.enter_context(tc.tile_pool(name="prep", bufs=3))
+        edges_in = ctx.enter_context(tc.tile_pool(name="edges_in", bufs=UNITS))
+        node_pool = ctx.enter_context(tc.tile_pool(name="node_pool", bufs=2))
+        front = ctx.enter_context(tc.tile_pool(name="front", bufs=3))
+        hidden = ctx.enter_context(tc.tile_pool(name="hidden", bufs=2))
+        result = ctx.enter_context(tc.tile_pool(name="result", bufs=4))
+        ps_t = ctx.enter_context(tc.psum_pool(name="ps_t", bufs=2))
+        ps_1 = ctx.enter_context(tc.psum_pool(name="ps_1", bufs=4))
+        ps_2 = ctx.enter_context(tc.psum_pool(name="ps_2", bufs=2))
+
+        def quantise(codes, scales, grouped):
+            nc.vector.quantize_mx(out=codes.bitcast(FP8X4), scales=scales, in_=grouped)
+
+        def mx_pass(acc, w_codes, w_scales, x_codes, x_scales, start, stop):
+            nc.tensor.matmul_mx(
+                out=acc,
+                lhsT=w_codes.bitcast(FP8X4),
+                lhsT_scale=w_scales,
+                rhs=x_codes.bitcast(FP8X4),
+                rhs_scale=x_scales,
+                start=start,
+                stop=stop,
+            )
+
+        def load_w1_half(half):
+            raw = prep.tile([P, PACK, FEAT], BF16, name="w_raw")
+            nc.sync.dma_start(
+                out=raw[:].rearrange("q (u e) m -> q u (e m)", u=2),
+                in_=W1_w[half * FEAT : (half + 1) * FEAT, :].rearrange("(u q e) m -> q u (e m)", u=2, e=2),
+            )
+            return raw
+
+        edge_tiles = {}
+
+        def load_unit(n):
+            edge_tiles[n] = edges_in.tile([P, SUBS * FEAT], BF16, name="edge_rows")
+            nc.sync.dma_start(out=edge_tiles[n][:], in_=edge_units[n // BLOCK_UNITS, n % BLOCK_UNITS])
+
+        b1_bf = consts.tile([P, PACK], BF16)
+        nc.scalar.dma_start(out=b1_bf[:], in_=W1_b.rearrange("(p t) -> p t", t=PACK))
+
+        w1v_raw = load_w1_half(0)
+        node_rows = consts.tile([P, 2 * FEAT], BF16)
+        nc.sync.dma_start(
+            out=node_rows[:].rearrange("p (a c) -> p a c", a=2),
+            in_=h_V.rearrange("b n c -> (b n) c").rearrange("(a p) c -> p a c", p=P),
+        )
+        load_unit(0)
+        w1e_raw = load_w1_half(1)
+        load_unit(1)
+        w2_raw = prep.tile([P, PACK, FEAT], BF16, name="w_raw")
+        nc.sync.dma_start(
+            out=w2_raw[:].rearrange("p j n -> p (j n)"), in_=W2_w.rearrange("(p j) n -> p (j n)", j=PACK)
+        )
+        b2_all = consts.tile([P, FEAT], BF16)
+        nc.sync.dma_start(out=b2_all[:], in_=W2_b.partition_broadcast(P))
+        for n in range(2, UNITS):
+            load_unit(n)
+
+        ident = consts.tile([P, P], F32)
+        make_identity(nc, ident[:])
+        warm = consts.tile([P, 2], F32)
+        nc.vector.memset(warm[:], 0.0)
+        nc.scalar.activation(out=warm[:, 1:2], in_=warm[:, 0:1], func=GELU)
+        b1 = consts.tile([P, PACK], F32)
+        nc.vector.tensor_copy(out=b1[:], in_=b1_bf[:])
+
+        def quantise_w1_half(raw, name):
+            grouped = prep.tile([P, FEAT * PACK], BF16, name="w_grouped", align_bytes=64)
+            nc.vector.tensor_copy(
+                out=grouped[:].rearrange("q (t p j) -> q t p j", t=PACK, j=PACK),
+                in_=raw[:].rearrange("q j (p t) -> q t p j", t=PACK),
+            )
+            codes = consts.tile([P, FEAT], U32, name=name + "_codes", align_bytes=64)
+            scales = consts.tile([P, FEAT], U8, name=name + "_scales", align_bytes=64)
+            quantise(codes[:], scales[:], grouped[:])
+            return codes, scales
+
+        w1v_codes, w1v_scales = quantise_w1_half(w1v_raw, "w1v")
+
+        node_words = node_rows[:].bitcast(F32)
+        node_t = ps_t.tile([P, 2, 2, P], F32, name="words_t")
+        for a in range(2):
+            for u in range(2):
+                nc.tensor.transpose(node_t[:, a, u, :], node_words[:, (2 * a + u) * P : (2 * a + u + 1) * P], ident[:])
+        node_grouped = consts.tile([P, NODES * COPIES * PACK], BF16, align_bytes=64)
+        node_grouped_words = node_grouped[:].bitcast(F32).rearrange("p (a r d u) -> p a r d u", a=2, d=COPIES, u=2)
+        for a in range(2):
+            nc.scalar.copy(
+                out=node_grouped_words[:, a],
+                in_=node_t[:, a].rearrange("p u r -> p r u").unsqueeze(2).to_broadcast([P, P, COPIES, 2]),
+            )
+        node_codes = consts.tile([P, NODES * COPIES], U32, align_bytes=64)
+        node_scales = consts.tile([P, NODES * COPIES], U8, align_bytes=64)
+        nc.vector.memset(node_scales[:].bitcast(I32), 0)
+        quantise(node_codes[:], node_scales[:], node_grouped[:])
+
+        w1e_codes, w1e_scales = quantise_w1_half(w1e_raw, "w1e")
+
+        node_operands = {}
+
+        def repeat_nodes(g):
+            cols = slice(g * P, (g + 1) * P)
+            codes = node_pool.tile([P, UNIT], U32, name="node_rep_codes", align_bytes=64)
+            scales = node_pool.tile([P, UNIT], U8, name="node_rep_scales", align_bytes=64)
+            nc.vector.tensor_copy(
+                out=codes[:].bitcast(I32).rearrange("p (a w) -> p a w", a=SUBS),
+                in_=node_codes[:, cols].bitcast(I32).unsqueeze(1).to_broadcast([P, SUBS, P]),
+            )
+            nc.vector.tensor_copy(
+                out=scales[:].bitcast(I32).rearrange("p (a w) -> p a w", a=SUBS),
+                in_=node_scales[:, cols].bitcast(I32).unsqueeze(1).to_broadcast([P, SUBS, P // 4]),
+            )
+            node_operands[g] = (codes, scales)
+
+        w2 = {}
+
+        def quantise_w2():
+            grouped = prep.tile([P, FEAT * PACK], BF16, name="w_grouped", align_bytes=64)
+            nc.vector.tensor_copy(
+                out=grouped[:].rearrange("p (c i j) -> p c j i", i=4, j=PACK),
+                in_=w2_raw[:].rearrange("p j (c i) -> p c j i", i=4),
+            )
+            w2["codes"] = consts.tile([P, FEAT], U32, name="w2_codes", align_bytes=64)
+            w2["scales"] = consts.tile([P, FEAT], U8, name="w2_scales", align_bytes=64)
+            quantise(w2["codes"][:], w2["scales"][:], grouped[:])
+
+        banks_t, edge_grouped, edge_mx, banks_1, planes, h1_grouped, h1_mx, banks_2, results = (
+            {}, {}, {}, {}, {}, {}, {}, {}, {},
+        )
+
+        def transpose_edges(n):
+            words = edge_tiles[n][:].bitcast(F32)
+            banks_t[n] = []
+            for b in range(2):
+                bank = ps_t.tile([P, 2, 2, P], F32, name="words_t")
+                for a in range(2):
+                    for u in range(2):
+                        first = ((2 * b + a) * 2 + u) * P
+                        nc.tensor.transpose(bank[:, a, u, :], words[:, first : first + P], ident[:])
+                banks_t[n].append(bank)
+
+        def group_edges(n):
+            edge_grouped[n] = front.tile([P, UNIT * PACK], BF16, name="edge_grouped", align_bytes=64)
+            grouped_words = edge_grouped[n][:].bitcast(F32).rearrange("p (a r u) -> p a r u", a=SUBS, u=2)
+            for b in range(2):
+                nc.scalar.copy(
+                    out=grouped_words[:, 2 * b : 2 * b + 2],
+                    in_=banks_t[n][b][:].rearrange("p a u r -> p a r u"),
+                )
+
+        def quantise_edges(n):
+            codes = front.tile([P, UNIT], U32, name="edge_codes", align_bytes=64)
+            scales = front.tile([P, UNIT], U8, name="edge_scales", align_bytes=64)
+            quantise(codes[:], scales[:], edge_grouped[n][:])
+            edge_mx[n] = (codes, scales)
+
+        def stage1_matmuls(n):
+            e_codes, e_scales = edge_mx[n]
+            v_codes, v_scales = node_operands[n // BLOCK_UNITS]
+            banks_1[n] = []
+            for t in range(PACK):
+                cols = slice(t * P, (t + 1) * P)
+                acc = ps_1.tile([P, UNIT], F32, name="acc1")
+                mx_pass(acc[:], w1e_codes[:, cols], w1e_scales[:, cols], e_codes[:], e_scales[:], True, False)
+                mx_pass(acc[:], w1v_codes[:, cols], w1v_scales[:, cols], v_codes[:], v_scales[:], False, True)
+                banks_1[n].append(acc)
+
+        def stage1_gelu(n):
+            planes[n] = hidden.tile([P, PACK, UNIT], BF16, name="h1_planes")
+            for t in range(PACK):
+                nc.scalar.activation(
+                    out=planes[n][:, t, :], in_=banks_1[n][t][:], func=GELU, bias=b1[:, t : t + 1], scale=1.0
+                )
+
+        def group_h1(n):
+            h1_grouped[n] = hidden.tile([P, UNIT * PACK], BF16, name="h1_grouped", align_bytes=64)
+            nc.vector.tensor_copy(
+                out=h1_grouped[n][:].rearrange("p (c i t) -> p c t i", i=4, t=PACK),
+                in_=planes[n][:].rearrange("p t (c i) -> p c t i", i=4),
+            )
+
+        def quantise_h1(n):
+            codes = hidden.tile([P, UNIT], U32, name="h1_codes", align_bytes=64)
+            scales = hidden.tile([P, UNIT], U8, name="h1_scales", align_bytes=64)
+            quantise(codes[:], scales[:], h1_grouped[n][:])
+            h1_mx[n] = (codes, scales)
+
+        def stage2_matmuls(n):
+            codes, scales = h1_mx[n]
+            banks_2[n] = []
+            for a in range(SUBS):
+                cols = slice(a * P, (a + 1) * P)
+                acc = ps_2.tile([P, FEAT], F32, name="acc2")
+                mx_pass(acc[:], codes[:, cols], scales[:, cols], w2["codes"][:], w2["scales"][:], True, True)
+                banks_2[n].append(acc)
+
+        def stage2_bias(n):
+            results[n] = result.tile([P, SUBS, FEAT], F32, name="z")
+            for a in range(SUBS):
+                nc.vector.tensor_tensor(out=results[n][:, a, :], in0=banks_2[n][a][:], in1=b2_all[:], op=ADD)
+
+        def stage2_gelu_and_store(n):
+            z = results[n][:].rearrange("p a m -> p (a m)")
+            nc.scalar.activation(out=z, in_=z, func=GELU)
+            nc.sync.dma_start(out=out_units[n // BLOCK_UNITS, n % BLOCK_UNITS], in_=z)
+
+        def in_range(n):
+            return 0 <= n < UNITS
+
+        for i in range(-3, UNITS + 1):
+            if in_range(i - 1):
+                stage2_bias(i - 1)
+            if in_range(i):
+                stage1_gelu(i)
+            if in_range(i + 3):
+                transpose_edges(i + 3)
+                group_edges(i + 3)
+            if in_range(i):
+                group_h1(i)
+            if in_range(i - 1):
+                stage2_gelu_and_store(i - 1)
+            if in_range(i + 2):
+                quantise_edges(i + 2)
+            if in_range(i + 1):
+                if (i + 1) % BLOCK_UNITS == 0:
+                    repeat_nodes((i + 1) // BLOCK_UNITS)
+                stage1_matmuls(i + 1)
+            if i == -1:
+                quantise_w2()
+            if in_range(i):
+                quantise_h1(i)
+                stage2_matmuls(i)

@@ -11,6 +11,7 @@ U8 = mybir.dt.uint8
 FP8X4 = mybir.dt.float8_e4m3fn_x4
 GELU = mybir.ActivationFunctionType.Gelu_apprx_tanh
 ADD = mybir.AluOpType.add
+MULT = mybir.AluOpType.mult
 
 P = 128
 PACK = 4
@@ -45,11 +46,12 @@ def tile_declayerj_pa_t_kernel(tc, h_V, h_E, W1_w, W1_b, W2_w, W2_b, out):
         edges_in = ctx.enter_context(tc.tile_pool(name="edges_in", bufs=UNITS))
         node_pool = ctx.enter_context(tc.tile_pool(name="node_pool", bufs=2))
         front = ctx.enter_context(tc.tile_pool(name="front", bufs=3))
-        hidden = ctx.enter_context(tc.tile_pool(name="hidden", bufs=2))
+        hidden = ctx.enter_context(tc.tile_pool(name="hidden", bufs=3))
         result = ctx.enter_context(tc.tile_pool(name="result", bufs=4))
         ps_t = ctx.enter_context(tc.psum_pool(name="ps_t", bufs=2))
-        ps_1 = ctx.enter_context(tc.psum_pool(name="ps_1", bufs=4))
-        ps_2 = ctx.enter_context(tc.psum_pool(name="ps_2", bufs=2))
+        ps_1 = ctx.enter_context(tc.psum_pool(name="ps_1", bufs=3))
+        ps_2 = ctx.enter_context(tc.psum_pool(name="ps_2", bufs=3))
+        ctx.enter_context(tc.manual_schedule())
 
         def quantise(codes, scales, grouped):
             nc.vector.quantize_mx(out=codes.bitcast(FP8X4), scales=scales, in_=grouped)
@@ -64,6 +66,9 @@ def tile_declayerj_pa_t_kernel(tc, h_V, h_E, W1_w, W1_b, W2_w, W2_b, out):
                 start=start,
                 stop=stop,
             )
+
+        def gpsimd_copy(dst, src):
+            nc.gpsimd.tensor_scalar(out=dst, in0=src, scalar1=1.0, scalar2=0.0, op0=MULT, op1=ADD)
 
         def load_w1_half(half):
             raw = prep.tile([P, PACK, FEAT], BF16, name="w_raw")
@@ -82,22 +87,23 @@ def tile_declayerj_pa_t_kernel(tc, h_V, h_E, W1_w, W1_b, W2_w, W2_b, out):
         b1_bf = consts.tile([P, PACK], BF16)
         nc.scalar.dma_start(out=b1_bf[:], in_=W1_b.rearrange("(p t) -> p t", t=PACK))
 
-        w1v_raw = load_w1_half(0)
         node_rows = consts.tile([P, 2 * FEAT], BF16)
         nc.sync.dma_start(
             out=node_rows[:].rearrange("p (a c) -> p a c", a=2),
             in_=h_V.rearrange("b n c -> (b n) c").rearrange("(a p) c -> p a c", p=P),
         )
         load_unit(0)
+        w1v_raw = load_w1_half(0)
         w1e_raw = load_w1_half(1)
         load_unit(1)
         w2_raw = prep.tile([P, PACK, FEAT], BF16, name="w_raw")
         nc.sync.dma_start(
             out=w2_raw[:].rearrange("p j n -> p (j n)"), in_=W2_w.rearrange("(p j) n -> p (j n)", j=PACK)
         )
+        load_unit(2)
         b2_all = consts.tile([P, FEAT], BF16)
         nc.sync.dma_start(out=b2_all[:], in_=W2_b.partition_broadcast(P))
-        for n in range(2, UNITS):
+        for n in range(3, UNITS):
             load_unit(n)
 
         ident = consts.tile([P, P], F32)
@@ -105,40 +111,51 @@ def tile_declayerj_pa_t_kernel(tc, h_V, h_E, W1_w, W1_b, W2_w, W2_b, out):
         warm = consts.tile([P, 2], F32)
         nc.vector.memset(warm[:], 0.0)
         nc.scalar.activation(out=warm[:, 1:2], in_=warm[:, 0:1], func=GELU)
-        b1 = consts.tile([P, PACK], F32)
-        nc.vector.tensor_copy(out=b1[:], in_=b1_bf[:])
 
         def quantise_w1_half(raw, name):
             grouped = prep.tile([P, FEAT * PACK], BF16, name="w_grouped", align_bytes=64)
-            nc.vector.tensor_copy(
-                out=grouped[:].rearrange("q (t p j) -> q t p j", t=PACK, j=PACK),
-                in_=raw[:].rearrange("q j (p t) -> q t p j", t=PACK),
-            )
+            grouped_by_tile = grouped[:].rearrange("q (t p j) -> q t p j", t=PACK, j=PACK)
+            raw_by_tile = raw[:].rearrange("q j (p t) -> q t p j", t=PACK)
+            nc.scalar.copy(out=grouped_by_tile[:, 0:2], in_=raw_by_tile[:, 0:2])
+            gpsimd_copy(grouped_by_tile[:, 2:4], raw_by_tile[:, 2:4])
             codes = consts.tile([P, FEAT], U32, name=name + "_codes", align_bytes=64)
             scales = consts.tile([P, FEAT], U8, name=name + "_scales", align_bytes=64)
             quantise(codes[:], scales[:], grouped[:])
             return codes, scales
 
-        w1v_codes, w1v_scales = quantise_w1_half(w1v_raw, "w1v")
+        w2 = {}
 
-        node_words = node_rows[:].bitcast(F32)
-        node_t = ps_t.tile([P, 2, 2, P], F32, name="words_t")
-        for a in range(2):
-            for u in range(2):
-                nc.tensor.transpose(node_t[:, a, u, :], node_words[:, (2 * a + u) * P : (2 * a + u + 1) * P], ident[:])
-        node_grouped = consts.tile([P, NODES * COPIES * PACK], BF16, align_bytes=64)
-        node_grouped_words = node_grouped[:].bitcast(F32).rearrange("p (a r d u) -> p a r d u", a=2, d=COPIES, u=2)
-        for a in range(2):
-            nc.scalar.copy(
-                out=node_grouped_words[:, a],
-                in_=node_t[:, a].rearrange("p u r -> p r u").unsqueeze(2).to_broadcast([P, P, COPIES, 2]),
+        def quantise_w2():
+            grouped = prep.tile([P, FEAT * PACK], BF16, name="w_grouped", align_bytes=64)
+            nc.vector.tensor_copy(
+                out=grouped[:].rearrange("p (c i j) -> p c j i", i=4, j=PACK),
+                in_=w2_raw[:].rearrange("p j (c i) -> p c j i", i=4),
             )
+            w2["codes"] = consts.tile([P, FEAT], U32, name="w2_codes", align_bytes=64)
+            w2["scales"] = consts.tile([P, FEAT], U8, name="w2_scales", align_bytes=64)
+            quantise(w2["codes"][:], w2["scales"][:], grouped[:])
+
         node_codes = consts.tile([P, NODES * COPIES], U32, align_bytes=64)
         node_scales = consts.tile([P, NODES * COPIES], U8, align_bytes=64)
-        nc.vector.memset(node_scales[:].bitcast(I32), 0)
-        quantise(node_codes[:], node_scales[:], node_grouped[:])
+        b1 = consts.tile([P, PACK], F32)
 
-        w1e_codes, w1e_scales = quantise_w1_half(w1e_raw, "w1e")
+        def quantise_nodes():
+            nc.vector.memset(node_scales[:].bitcast(I32), 0)
+            node_words = node_rows[:].bitcast(F32)
+            node_t = ps_t.tile([P, 2, 2, P], F32, name="words_t")
+            for a in range(2):
+                for u in range(2):
+                    first = (2 * a + u) * P
+                    nc.tensor.transpose(node_t[:, a, u, :], node_words[:, first : first + P], ident[:])
+            node_grouped = consts.tile([P, NODES * COPIES * PACK], BF16, align_bytes=64)
+            grouped_words = node_grouped[:].bitcast(F32).rearrange("p (a r d u) -> p a r d u", a=2, d=COPIES, u=2)
+            twice = [
+                node_t[:, a].rearrange("p u r -> p r u").unsqueeze(2).to_broadcast([P, P, COPIES, 2]) for a in range(2)
+            ]
+            nc.scalar.copy(out=grouped_words[:, 0], in_=twice[0])
+            nc.vector.tensor_copy(out=grouped_words[:, 1], in_=twice[1])
+            nc.vector.tensor_copy(out=b1[:], in_=b1_bf[:])
+            quantise(node_codes[:], node_scales[:], node_grouped[:])
 
         node_operands = {}
 
@@ -156,21 +173,10 @@ def tile_declayerj_pa_t_kernel(tc, h_V, h_E, W1_w, W1_b, W2_w, W2_b, out):
             )
             node_operands[g] = (codes, scales)
 
-        w2 = {}
-
-        def quantise_w2():
-            grouped = prep.tile([P, FEAT * PACK], BF16, name="w_grouped", align_bytes=64)
-            nc.vector.tensor_copy(
-                out=grouped[:].rearrange("p (c i j) -> p c j i", i=4, j=PACK),
-                in_=w2_raw[:].rearrange("p j (c i) -> p c j i", i=4),
-            )
-            w2["codes"] = consts.tile([P, FEAT], U32, name="w2_codes", align_bytes=64)
-            w2["scales"] = consts.tile([P, FEAT], U8, name="w2_scales", align_bytes=64)
-            quantise(w2["codes"][:], w2["scales"][:], grouped[:])
-
         banks_t, edge_grouped, edge_mx, banks_1, planes, h1_grouped, h1_mx, banks_2, results = (
             {}, {}, {}, {}, {}, {}, {}, {}, {},
         )
+        w1 = {}
 
         def transpose_edges(n):
             words = edge_tiles[n][:].bitcast(F32)
@@ -186,11 +192,8 @@ def tile_declayerj_pa_t_kernel(tc, h_V, h_E, W1_w, W1_b, W2_w, W2_b, out):
         def group_edges(n):
             edge_grouped[n] = front.tile([P, UNIT * PACK], BF16, name="edge_grouped", align_bytes=64)
             grouped_words = edge_grouped[n][:].bitcast(F32).rearrange("p (a r u) -> p a r u", a=SUBS, u=2)
-            for b in range(2):
-                nc.scalar.copy(
-                    out=grouped_words[:, 2 * b : 2 * b + 2],
-                    in_=banks_t[n][b][:].rearrange("p a u r -> p a r u"),
-                )
+            nc.scalar.copy(out=grouped_words[:, 0:2], in_=banks_t[n][0][:].rearrange("p a u r -> p a r u"))
+            nc.vector.tensor_copy(out=grouped_words[:, 2:4], in_=banks_t[n][1][:].rearrange("p a u r -> p a r u"))
 
         def quantise_edges(n):
             codes = front.tile([P, UNIT], U32, name="edge_codes", align_bytes=64)
@@ -201,6 +204,8 @@ def tile_declayerj_pa_t_kernel(tc, h_V, h_E, W1_w, W1_b, W2_w, W2_b, out):
         def stage1_matmuls(n):
             e_codes, e_scales = edge_mx[n]
             v_codes, v_scales = node_operands[n // BLOCK_UNITS]
+            w1e_codes, w1e_scales = w1["edges"]
+            w1v_codes, w1v_scales = w1["nodes"]
             banks_1[n] = []
             for t in range(PACK):
                 cols = slice(t * P, (t + 1) * P)
@@ -218,10 +223,11 @@ def tile_declayerj_pa_t_kernel(tc, h_V, h_E, W1_w, W1_b, W2_w, W2_b, out):
 
         def group_h1(n):
             h1_grouped[n] = hidden.tile([P, UNIT * PACK], BF16, name="h1_grouped", align_bytes=64)
-            nc.vector.tensor_copy(
-                out=h1_grouped[n][:].rearrange("p (c i t) -> p c t i", i=4, t=PACK),
-                in_=planes[n][:].rearrange("p t (c i) -> p c t i", i=4),
-            )
+            for a in range(SUBS):
+                gpsimd_copy(
+                    h1_grouped[n][:, a * FEAT : (a + 1) * FEAT].rearrange("p (r t) -> p r t", t=PACK),
+                    planes[n][:, :, a * P : (a + 1) * P].rearrange("p t r -> p r t"),
+                )
 
         def quantise_h1(n):
             codes = hidden.tile([P, UNIT], U32, name="h1_codes", align_bytes=64)
@@ -239,38 +245,57 @@ def tile_declayerj_pa_t_kernel(tc, h_V, h_E, W1_w, W1_b, W2_w, W2_b, out):
                 banks_2[n].append(acc)
 
         def stage2_bias(n):
-            results[n] = result.tile([P, SUBS, FEAT], F32, name="z")
+            results[n] = result.tile([P, SUBS * FEAT], F32, name="z")
             for a in range(SUBS):
-                nc.vector.tensor_tensor(out=results[n][:, a, :], in0=banks_2[n][a][:], in1=b2_all[:], op=ADD)
+                nc.vector.tensor_tensor(
+                    out=results[n][:, a * FEAT : (a + 1) * FEAT], in0=banks_2[n][a][:], in1=b2_all[:], op=ADD
+                )
 
         def stage2_gelu_and_store(n):
-            z = results[n][:].rearrange("p a m -> p (a m)")
-            nc.scalar.activation(out=z, in_=z, func=GELU)
-            nc.sync.dma_start(out=out_units[n // BLOCK_UNITS, n % BLOCK_UNITS], in_=z)
+            pieces = SUBS if n == UNITS - 1 else 1
+            width = SUBS * FEAT // pieces
+            for k in range(pieces):
+                cols = slice(k * width, (k + 1) * width)
+                nc.scalar.activation(out=results[n][:, cols], in_=results[n][:, cols], func=GELU)
+                nc.sync.dma_start(out=out_units[n // BLOCK_UNITS, n % BLOCK_UNITS][:, cols], in_=results[n][:, cols])
+
+        quantise_nodes()
+        transpose_edges(0)
+        group_edges(0)
+        repeat_nodes(0)
+        transpose_edges(1)
+        quantise_edges(0)
+        w1["nodes"] = quantise_w1_half(w1v_raw, "w1v")
+        w1["edges"] = quantise_w1_half(w1e_raw, "w1e")
+        group_edges(1)
+        stage1_matmuls(0)
+        transpose_edges(2)
 
         def in_range(n):
             return 0 <= n < UNITS
 
-        for i in range(-3, UNITS + 1):
-            if in_range(i - 1):
-                stage2_bias(i - 1)
+        for i in range(UNITS + 2):
             if in_range(i):
                 stage1_gelu(i)
-            if in_range(i + 3):
-                transpose_edges(i + 3)
-                group_edges(i + 3)
+            if in_range(i - 1):
+                quantise_h1(i - 1)
+            if in_range(i + 1):
+                quantise_edges(i + 1)
+            if i == 0:
+                quantise_w2()
+            if in_range(i - 1):
+                stage2_matmuls(i - 1)
+            if in_range(i + 2):
+                group_edges(i + 2)
+            if in_range(i - 1):
+                stage2_bias(i - 1)
+            if in_range(i + 2) and (i + 2) % BLOCK_UNITS == 0:
+                repeat_nodes((i + 2) // BLOCK_UNITS)
             if in_range(i):
                 group_h1(i)
-            if in_range(i - 1):
-                stage2_gelu_and_store(i - 1)
-            if in_range(i + 2):
-                quantise_edges(i + 2)
+            if in_range(i - 2):
+                stage2_gelu_and_store(i - 2)
+            if in_range(i + 3):
+                transpose_edges(i + 3)
             if in_range(i + 1):
-                if (i + 1) % BLOCK_UNITS == 0:
-                    repeat_nodes((i + 1) // BLOCK_UNITS)
                 stage1_matmuls(i + 1)
-            if i == -1:
-                quantise_w2()
-            if in_range(i):
-                quantise_h1(i)
-                stage2_matmuls(i)

@@ -125,12 +125,12 @@ def tile_declayerj_pa_t_kernel(tc, h_V, h_E, W1_w, W1_b, W2_w, W2_b, out):
 
         w2 = {}
 
+        def group_w2():
+            w2["grouped"] = prep.tile([P, FEAT * PACK], BF16, name="w_grouped", align_bytes=64)
+            gpsimd_copy(w2["grouped"][:].rearrange("p (n j) -> p n j", j=PACK), w2_raw[:].rearrange("p j n -> p n j"))
+
         def quantise_w2():
-            grouped = prep.tile([P, FEAT * PACK], BF16, name="w_grouped", align_bytes=64)
-            nc.vector.tensor_copy(
-                out=grouped[:].rearrange("p (c i j) -> p c j i", i=4, j=PACK),
-                in_=w2_raw[:].rearrange("p j (c i) -> p c j i", i=4),
-            )
+            grouped = w2["grouped"]
             w2["codes"] = consts.tile([P, FEAT], U32, name="w2_codes", align_bytes=64)
             w2["scales"] = consts.tile([P, FEAT], U8, name="w2_scales", align_bytes=64)
             quantise(w2["codes"][:], w2["scales"][:], grouped[:])
@@ -153,7 +153,7 @@ def tile_declayerj_pa_t_kernel(tc, h_V, h_E, W1_w, W1_b, W2_w, W2_b, out):
                 node_t[:, a].rearrange("p u r -> p r u").unsqueeze(2).to_broadcast([P, P, COPIES, 2]) for a in range(2)
             ]
             nc.scalar.copy(out=grouped_words[:, 0], in_=twice[0])
-            nc.vector.tensor_copy(out=grouped_words[:, 1], in_=twice[1])
+            nc.scalar.copy(out=grouped_words[:, 1], in_=twice[1])
             nc.vector.tensor_copy(out=b1[:], in_=b1_bf[:])
             quantise(node_codes[:], node_scales[:], node_grouped[:])
 
@@ -189,11 +189,13 @@ def tile_declayerj_pa_t_kernel(tc, h_V, h_E, W1_w, W1_b, W2_w, W2_b, out):
                         nc.tensor.transpose(bank[:, a, u, :], words[:, first : first + P], ident[:])
                 banks_t[n].append(bank)
 
-        def group_edges(n):
-            edge_grouped[n] = front.tile([P, UNIT * PACK], BF16, name="edge_grouped", align_bytes=64)
+        def group_edges(n, b):
+            if b == 0:
+                edge_grouped[n] = front.tile([P, UNIT * PACK], BF16, name="edge_grouped", align_bytes=64)
             grouped_words = edge_grouped[n][:].bitcast(F32).rearrange("p (a r u) -> p a r u", a=SUBS, u=2)
-            nc.scalar.copy(out=grouped_words[:, 0:2], in_=banks_t[n][0][:].rearrange("p a u r -> p a r u"))
-            nc.vector.tensor_copy(out=grouped_words[:, 2:4], in_=banks_t[n][1][:].rearrange("p a u r -> p a r u"))
+            nc.vector.tensor_copy(
+                out=grouped_words[:, 2 * b : 2 * b + 2], in_=banks_t[n][b][:].rearrange("p a u r -> p a r u")
+            )
 
         def quantise_edges(n):
             codes = front.tile([P, UNIT], U32, name="edge_codes", align_bytes=64)
@@ -229,73 +231,89 @@ def tile_declayerj_pa_t_kernel(tc, h_V, h_E, W1_w, W1_b, W2_w, W2_b, out):
                     planes[n][:, :, a * P : (a + 1) * P].rearrange("p t r -> p r t"),
                 )
 
-        def quantise_h1(n):
-            codes = hidden.tile([P, UNIT], U32, name="h1_codes", align_bytes=64)
-            scales = hidden.tile([P, UNIT], U8, name="h1_scales", align_bytes=64)
-            quantise(codes[:], scales[:], h1_grouped[n][:])
-            h1_mx[n] = (codes, scales)
-
-        def stage2_matmuls(n):
+        def quantise_h1(n, first, last):
+            if first == 0:
+                h1_mx[n] = (
+                    hidden.tile([P, UNIT], U32, name="h1_codes", align_bytes=64),
+                    hidden.tile([P, UNIT], U8, name="h1_scales", align_bytes=64),
+                )
+                banks_2[n] = {}
+                results[n] = result.tile([P, SUBS * FEAT], F32, name="z")
             codes, scales = h1_mx[n]
-            banks_2[n] = []
-            for a in range(SUBS):
-                cols = slice(a * P, (a + 1) * P)
-                acc = ps_2.tile([P, FEAT], F32, name="acc2")
-                mx_pass(acc[:], codes[:, cols], scales[:, cols], w2["codes"][:], w2["scales"][:], True, True)
-                banks_2[n].append(acc)
+            cols = slice(first * P, last * P)
+            quantise(codes[:, cols], scales[:, cols], h1_grouped[n][:, first * FEAT : last * FEAT])
 
-        def stage2_bias(n):
-            results[n] = result.tile([P, SUBS * FEAT], F32, name="z")
-            for a in range(SUBS):
+        def stage2_matmuls(n, first, last):
+            codes, scales = h1_mx[n]
+            for a in range(first, last):
+                cols = slice(a * P, (a + 1) * P)
+                banks_2[n][a] = ps_2.tile([P, FEAT], F32, name="acc2")
+                mx_pass(banks_2[n][a][:], codes[:, cols], scales[:, cols], w2["codes"][:], w2["scales"][:], True, True)
+
+        def stage2_bias(n, first, last):
+            for a in range(first, last):
                 nc.vector.tensor_tensor(
                     out=results[n][:, a * FEAT : (a + 1) * FEAT], in0=banks_2[n][a][:], in1=b2_all[:], op=ADD
                 )
 
-        def stage2_gelu_and_store(n):
-            pieces = SUBS if n == UNITS - 1 else 1
-            width = SUBS * FEAT // pieces
-            for k in range(pieces):
-                cols = slice(k * width, (k + 1) * width)
-                nc.scalar.activation(out=results[n][:, cols], in_=results[n][:, cols], func=GELU)
-                nc.sync.dma_start(out=out_units[n // BLOCK_UNITS, n % BLOCK_UNITS][:, cols], in_=results[n][:, cols])
+        def stage2_gelu_and_store(n, first, last):
+            cols = slice(first * FEAT, last * FEAT)
+            nc.scalar.activation(out=results[n][:, cols], in_=results[n][:, cols], func=GELU)
+            nc.sync.dma_start(out=out_units[n // BLOCK_UNITS, n % BLOCK_UNITS][:, cols], in_=results[n][:, cols])
 
         quantise_nodes()
         transpose_edges(0)
-        group_edges(0)
+        group_edges(0, 0)
+        group_edges(0, 1)
         repeat_nodes(0)
         transpose_edges(1)
         quantise_edges(0)
         w1["nodes"] = quantise_w1_half(w1v_raw, "w1v")
         w1["edges"] = quantise_w1_half(w1e_raw, "w1e")
-        group_edges(1)
+        group_edges(1, 0)
+        group_edges(1, 1)
+        group_w2()
         stage1_matmuls(0)
         transpose_edges(2)
 
         def in_range(n):
             return 0 <= n < UNITS
 
-        for i in range(UNITS + 2):
+        def whole(n):
+            return 0 <= n < UNITS - 1
+
+        for i in range(UNITS + 1):
             if in_range(i):
                 stage1_gelu(i)
-            if in_range(i - 1):
-                quantise_h1(i - 1)
+            if whole(i - 1):
+                quantise_h1(i - 1, 0, SUBS)
             if in_range(i + 1):
                 quantise_edges(i + 1)
             if i == 0:
                 quantise_w2()
-            if in_range(i - 1):
-                stage2_matmuls(i - 1)
+            if whole(i - 1):
+                stage2_matmuls(i - 1, 0, SUBS)
             if in_range(i + 2):
-                group_edges(i + 2)
-            if in_range(i - 1):
-                stage2_bias(i - 1)
+                group_edges(i + 2, 0)
+            if whole(i - 1):
+                stage2_bias(i - 1, 0, SUBS)
+            if in_range(i + 2):
+                group_edges(i + 2, 1)
             if in_range(i + 2) and (i + 2) % BLOCK_UNITS == 0:
                 repeat_nodes((i + 2) // BLOCK_UNITS)
             if in_range(i):
                 group_h1(i)
-            if in_range(i - 2):
-                stage2_gelu_and_store(i - 2)
-            if in_range(i + 3):
-                transpose_edges(i + 3)
+            if whole(i - 2):
+                stage2_gelu_and_store(i - 2, 0, SUBS)
             if in_range(i + 1):
                 stage1_matmuls(i + 1)
+            if in_range(i + 3):
+                transpose_edges(i + 3)
+
+        for a in range(SUBS + 1):
+            if a < SUBS:
+                quantise_h1(UNITS - 1, a, a + 1)
+                stage2_matmuls(UNITS - 1, a, a + 1)
+            if a > 0:
+                stage2_bias(UNITS - 1, a - 1, a)
+                stage2_gelu_and_store(UNITS - 1, a - 1, a)

@@ -212,8 +212,8 @@ def tile_declayerj_pa_t_kernel(tc, h_V, h_E, W1_w, W1_b, W2_w, W2_b, out):
             for t in range(PACK):
                 cols = slice(t * P, (t + 1) * P)
                 acc = ps_1.tile([P, UNIT], F32, name="acc1")
-                mx_pass(acc[:], w1e_codes[:, cols], w1e_scales[:, cols], e_codes[:], e_scales[:], True, False)
-                mx_pass(acc[:], w1v_codes[:, cols], w1v_scales[:, cols], v_codes[:], v_scales[:], False, True)
+                mx_pass(acc[:], w1v_codes[:, cols], w1v_scales[:, cols], v_codes[:], v_scales[:], True, False)
+                mx_pass(acc[:], w1e_codes[:, cols], w1e_scales[:, cols], e_codes[:], e_scales[:], False, True)
                 banks_1[n].append(acc)
 
         def stage1_gelu(n):
@@ -225,6 +225,12 @@ def tile_declayerj_pa_t_kernel(tc, h_V, h_E, W1_w, W1_b, W2_w, W2_b, out):
 
         def group_h1(n):
             h1_grouped[n] = hidden.tile([P, UNIT * PACK], BF16, name="h1_grouped", align_bytes=64)
+            if n == 0:
+                nc.vector.tensor_copy(
+                    out=h1_grouped[n][:].rearrange("p (c i t) -> p c t i", i=4, t=PACK),
+                    in_=planes[n][:].rearrange("p t (c i) -> p c t i", i=4),
+                )
+                return
             for a in range(SUBS):
                 gpsimd_copy(
                     h1_grouped[n][:, a * FEAT : (a + 1) * FEAT].rearrange("p (r t) -> p r t", t=PACK),

@@ -22,10 +22,8 @@ ROWS = NODES * EDGES
 UNIT = 512
 SUBS = UNIT // P
 UNITS = ROWS // UNIT
-BLOCK_UNITS = 4
+BLOCK_UNITS = 8
 BLOCKS = UNITS // BLOCK_UNITS
-BLOCK_NODES = NODES // BLOCKS
-COPIES = P // BLOCK_NODES
 
 FLOPS = 2 * FEAT * FEAT * (NODES + 2 * ROWS)
 
@@ -45,7 +43,7 @@ def tile_declayerj_pa_t_kernel(tc, h_V, h_E, W1_w, W1_b, W2_w, W2_b, out):
         prep = ctx.enter_context(tc.tile_pool(name="prep", bufs=3))
         edges_in = ctx.enter_context(tc.tile_pool(name="edges_in", bufs=UNITS))
         node_pool = ctx.enter_context(tc.tile_pool(name="node_pool", bufs=2))
-        front = ctx.enter_context(tc.tile_pool(name="front", bufs=3))
+        front = ctx.enter_context(tc.tile_pool(name="front", bufs=4))
         hidden = ctx.enter_context(tc.tile_pool(name="hidden", bufs=3))
         result = ctx.enter_context(tc.tile_pool(name="result", bufs=4))
         ps_t = ctx.enter_context(tc.psum_pool(name="ps_t", bufs=2))
@@ -112,22 +110,32 @@ def tile_declayerj_pa_t_kernel(tc, h_V, h_E, W1_w, W1_b, W2_w, W2_b, out):
         nc.vector.memset(warm[:], 0.0)
         nc.scalar.activation(out=warm[:, 1:2], in_=warm[:, 0:1], func=GELU)
 
-        def quantise_w1_half(raw, name):
-            grouped = prep.tile([P, FEAT * PACK], BF16, name="w_grouped", align_bytes=64)
-            grouped_by_tile = grouped[:].rearrange("q (t p j) -> q t p j", t=PACK, j=PACK)
-            raw_by_tile = raw[:].rearrange("q j (p t) -> q t p j", t=PACK)
-            nc.scalar.copy(out=grouped_by_tile[:, 0:2], in_=raw_by_tile[:, 0:2])
-            gpsimd_copy(grouped_by_tile[:, 2:4], raw_by_tile[:, 2:4])
-            codes = consts.tile([P, FEAT], U32, name=name + "_codes", align_bytes=64)
-            scales = consts.tile([P, FEAT], U8, name=name + "_scales", align_bytes=64)
-            quantise(codes[:], scales[:], grouped[:])
-            return codes, scales
+        w1 = {}
+        for half in ("nodes", "edges"):
+            w1[half] = (
+                prep.tile([P, FEAT * PACK], BF16, name="w_grouped", align_bytes=64),
+                consts.tile([P, FEAT], U32, name="w1_codes_" + half, align_bytes=64),
+                consts.tile([P, FEAT], U8, name="w1_scales_" + half, align_bytes=64),
+            )
+
+        def group_w1(half, raw, t, copy):
+            copy(
+                out=w1[half][0][:, t * FEAT : (t + 1) * FEAT].rearrange("q (p j) -> q p j", j=PACK),
+                in_=raw[:].rearrange("q j (p t) -> q t p j", t=PACK)[:, t],
+            )
+
+        def quantise_w1(half, t):
+            grouped, codes, scales = w1[half]
+            cols = slice(t * P, (t + 1) * P)
+            quantise(codes[:, cols], scales[:, cols], grouped[:, t * FEAT : (t + 1) * FEAT])
 
         w2 = {}
 
         def group_w2():
             w2["grouped"] = prep.tile([P, FEAT * PACK], BF16, name="w_grouped", align_bytes=64)
-            gpsimd_copy(w2["grouped"][:].rearrange("p (n j) -> p n j", j=PACK), w2_raw[:].rearrange("p j n -> p n j"))
+            nc.vector.tensor_copy(
+                out=w2["grouped"][:].rearrange("p (n j) -> p n j", j=PACK), in_=w2_raw[:].rearrange("p j n -> p n j")
+            )
 
         def quantise_w2():
             grouped = w2["grouped"]
@@ -135,11 +143,11 @@ def tile_declayerj_pa_t_kernel(tc, h_V, h_E, W1_w, W1_b, W2_w, W2_b, out):
             w2["scales"] = consts.tile([P, FEAT], U8, name="w2_scales", align_bytes=64)
             quantise(w2["codes"][:], w2["scales"][:], grouped[:])
 
-        node_codes = consts.tile([P, NODES * COPIES], U32, align_bytes=64)
-        node_scales = consts.tile([P, NODES * COPIES], U8, align_bytes=64)
-        b1 = consts.tile([P, PACK], F32)
+        node_codes = consts.tile([P, NODES], U32, align_bytes=64)
+        node_scales = consts.tile([P, NODES], U8, align_bytes=64)
+        node_grouped = consts.tile([P, NODES * PACK], BF16, align_bytes=64)
 
-        def quantise_nodes():
+        def group_nodes():
             nc.vector.memset(node_scales[:].bitcast(I32), 0)
             node_words = node_rows[:].bitcast(F32)
             node_t = ps_t.tile([P, 2, 2, P], F32, name="words_t")
@@ -147,15 +155,10 @@ def tile_declayerj_pa_t_kernel(tc, h_V, h_E, W1_w, W1_b, W2_w, W2_b, out):
                 for u in range(2):
                     first = (2 * a + u) * P
                     nc.tensor.transpose(node_t[:, a, u, :], node_words[:, first : first + P], ident[:])
-            node_grouped = consts.tile([P, NODES * COPIES * PACK], BF16, align_bytes=64)
-            grouped_words = node_grouped[:].bitcast(F32).rearrange("p (a r d u) -> p a r d u", a=2, d=COPIES, u=2)
-            twice = [
-                node_t[:, a].rearrange("p u r -> p r u").unsqueeze(2).to_broadcast([P, P, COPIES, 2]) for a in range(2)
-            ]
-            nc.scalar.copy(out=grouped_words[:, 0], in_=twice[0])
-            nc.scalar.copy(out=grouped_words[:, 1], in_=twice[1])
-            nc.vector.tensor_copy(out=b1[:], in_=b1_bf[:])
-            quantise(node_codes[:], node_scales[:], node_grouped[:])
+            nc.scalar.copy(
+                out=node_grouped[:].bitcast(F32).rearrange("p (a r u) -> p a r u", a=2, u=2),
+                in_=node_t[:].rearrange("p a u r -> p a r u"),
+            )
 
         node_operands = {}
 
@@ -176,8 +179,6 @@ def tile_declayerj_pa_t_kernel(tc, h_V, h_E, W1_w, W1_b, W2_w, W2_b, out):
         banks_t, edge_grouped, edge_mx, banks_1, planes, h1_grouped, h1_mx, banks_2, results = (
             {}, {}, {}, {}, {}, {}, {}, {}, {},
         )
-        w1 = {}
-
         def transpose_edges(n):
             words = edge_tiles[n][:].bitcast(F32)
             banks_t[n] = []
@@ -189,13 +190,11 @@ def tile_declayerj_pa_t_kernel(tc, h_V, h_E, W1_w, W1_b, W2_w, W2_b, out):
                         nc.tensor.transpose(bank[:, a, u, :], words[:, first : first + P], ident[:])
                 banks_t[n].append(bank)
 
-        def group_edges(n, b):
+        def group_edges(n, b, copy=nc.vector.tensor_copy):
             if b == 0:
                 edge_grouped[n] = front.tile([P, UNIT * PACK], BF16, name="edge_grouped", align_bytes=64)
             grouped_words = edge_grouped[n][:].bitcast(F32).rearrange("p (a r u) -> p a r u", a=SUBS, u=2)
-            nc.vector.tensor_copy(
-                out=grouped_words[:, 2 * b : 2 * b + 2], in_=banks_t[n][b][:].rearrange("p a u r -> p a r u")
-            )
+            copy(out=grouped_words[:, 2 * b : 2 * b + 2], in_=banks_t[n][b][:].rearrange("p a u r -> p a r u"))
 
         def quantise_edges(n):
             codes = front.tile([P, UNIT], U32, name="edge_codes", align_bytes=64)
@@ -203,24 +202,23 @@ def tile_declayerj_pa_t_kernel(tc, h_V, h_E, W1_w, W1_b, W2_w, W2_b, out):
             quantise(codes[:], scales[:], edge_grouped[n][:])
             edge_mx[n] = (codes, scales)
 
-        def stage1_matmuls(n):
+        def stage1_matmuls(n, tiles=range(PACK)):
             e_codes, e_scales = edge_mx[n]
             v_codes, v_scales = node_operands[n // BLOCK_UNITS]
-            w1e_codes, w1e_scales = w1["edges"]
-            w1v_codes, w1v_scales = w1["nodes"]
-            banks_1[n] = []
-            for t in range(PACK):
+            w1e_codes, w1e_scales = w1["edges"][1:]
+            w1v_codes, w1v_scales = w1["nodes"][1:]
+            for t in tiles:
                 cols = slice(t * P, (t + 1) * P)
                 acc = ps_1.tile([P, UNIT], F32, name="acc1")
                 mx_pass(acc[:], w1v_codes[:, cols], w1v_scales[:, cols], v_codes[:], v_scales[:], True, False)
                 mx_pass(acc[:], w1e_codes[:, cols], w1e_scales[:, cols], e_codes[:], e_scales[:], False, True)
-                banks_1[n].append(acc)
+                banks_1[n, t] = acc
 
         def stage1_gelu(n):
             planes[n] = hidden.tile([P, PACK, UNIT], BF16, name="h1_planes")
             for t in range(PACK):
                 nc.scalar.activation(
-                    out=planes[n][:, t, :], in_=banks_1[n][t][:], func=GELU, bias=b1[:, t : t + 1], scale=1.0
+                    out=planes[n][:, t, :], in_=banks_1[n, t][:], func=GELU, bias=b1_bf[:, t : t + 1], scale=1.0
                 )
 
         def group_h1(n):
@@ -267,20 +265,38 @@ def tile_declayerj_pa_t_kernel(tc, h_V, h_E, W1_w, W1_b, W2_w, W2_b, out):
             nc.scalar.activation(out=results[n][:, cols], in_=results[n][:, cols], func=GELU)
             nc.sync.dma_start(out=out_units[n // BLOCK_UNITS, n % BLOCK_UNITS][:, cols], in_=results[n][:, cols])
 
-        quantise_nodes()
+        group_nodes()
         transpose_edges(0)
-        group_edges(0, 0)
+        quantise(node_codes[:], node_scales[:], node_grouped[:])
+        group_edges(0, 0, nc.scalar.copy)
         group_edges(0, 1)
         repeat_nodes(0)
-        transpose_edges(1)
         quantise_edges(0)
-        w1["nodes"] = quantise_w1_half(w1v_raw, "w1v")
-        w1["edges"] = quantise_w1_half(w1e_raw, "w1e")
-        group_edges(1, 0)
-        group_edges(1, 1)
-        group_w2()
-        stage1_matmuls(0)
+        for half, raw in (("nodes", w1v_raw), ("edges", w1e_raw)):
+            for t in (0, 1):
+                group_w1(half, raw, t, nc.vector.tensor_copy)
+            for t in (2, 3):
+                group_w1(half, raw, t, nc.scalar.copy)
+            for t in range(PACK):
+                quantise_w1(half, t)
+        transpose_edges(1)
+        group_edges(1, 0, nc.scalar.copy)
+        group_edges(1, 1, nc.scalar.copy)
+        stage1_matmuls(0, range(3))
         transpose_edges(2)
+        stage1_matmuls(0, [3])
+        quantise_edges(1)
+        group_w2()
+        group_edges(2, 0)
+        group_edges(2, 1)
+        stage1_gelu(0)
+        stage1_matmuls(1, range(2))
+        transpose_edges(3)
+        stage1_matmuls(1, range(2, 4))
+        quantise_w2()
+        quantise_edges(2)
+        group_h1(0)
+        group_edges(3, 0)
 
         def in_range(n):
             return 0 <= n < UNITS
@@ -288,33 +304,36 @@ def tile_declayerj_pa_t_kernel(tc, h_V, h_E, W1_w, W1_b, W2_w, W2_b, out):
         def whole(n):
             return 0 <= n < UNITS - 1
 
-        for i in range(UNITS + 1):
+        for i in range(1, UNITS + 1):
             if in_range(i):
                 stage1_gelu(i)
             if whole(i - 1):
                 quantise_h1(i - 1, 0, SUBS)
-            if in_range(i + 1):
-                quantise_edges(i + 1)
-            if i == 0:
-                quantise_w2()
+            if in_range(i + 2):
+                if i == 1:
+                    group_edges(i + 2, 1)
+                quantise_edges(i + 2)
+            if in_range(i + 1) and i == 1:
+                stage1_matmuls(i + 1)
+                transpose_edges(i + 3)
             if whole(i - 1):
                 stage2_matmuls(i - 1, 0, SUBS)
-            if in_range(i + 2):
-                group_edges(i + 2, 0)
+            if in_range(i + 3):
+                group_edges(i + 3, 0)
             if whole(i - 1):
                 stage2_bias(i - 1, 0, SUBS)
-            if in_range(i + 2):
-                group_edges(i + 2, 1)
-            if in_range(i + 2) and (i + 2) % BLOCK_UNITS == 0:
-                repeat_nodes((i + 2) // BLOCK_UNITS)
+            if in_range(i + 3):
+                group_edges(i + 3, 1)
+            if i == 1:
+                repeat_nodes(1)
             if in_range(i):
                 group_h1(i)
             if whole(i - 2):
                 stage2_gelu_and_store(i - 2, 0, SUBS)
-            if in_range(i + 1):
+            if in_range(i + 1) and i > 1:
                 stage1_matmuls(i + 1)
-            if in_range(i + 3):
-                transpose_edges(i + 3)
+            if in_range(i + 4):
+                transpose_edges(i + 4)
 
         for a in range(SUBS + 1):
             if a < SUBS:

@@ -214,26 +214,26 @@ def tile_declayerj_pa_t_kernel(tc, h_V, h_E, W1_w, W1_b, W2_w, W2_b, out):
                 mx_pass(acc[:], w1e_codes[:, cols], w1e_scales[:, cols], e_codes[:], e_scales[:], False, True)
                 banks_1[n, t] = acc
 
-        def stage1_gelu(n):
-            planes[n] = hidden.tile([P, PACK, UNIT], BF16, name="h1_planes")
-            for t in range(PACK):
-                nc.scalar.activation(
-                    out=planes[n][:, t, :], in_=banks_1[n, t][:], func=GELU, bias=b1_bf[:, t : t + 1], scale=1.0
-                )
+        def stage1_gelu(n, t):
+            if t == 0:
+                planes[n] = hidden.tile([P, PACK, UNIT], BF16, name="h1_planes")
+            nc.scalar.activation(
+                out=planes[n][:, t, :], in_=banks_1[n, t][:], func=GELU, bias=b1_bf[:, t : t + 1], scale=1.0
+            )
 
-        def group_h1(n):
-            h1_grouped[n] = hidden.tile([P, UNIT * PACK], BF16, name="h1_grouped", align_bytes=64)
-            if n == 0:
-                nc.vector.tensor_copy(
-                    out=h1_grouped[n][:].rearrange("p (c i t) -> p c t i", i=4, t=PACK),
-                    in_=planes[n][:].rearrange("p t (c i) -> p c t i", i=4),
-                )
-                return
-            for a in range(SUBS):
-                gpsimd_copy(
-                    h1_grouped[n][:, a * FEAT : (a + 1) * FEAT].rearrange("p (r t) -> p r t", t=PACK),
-                    planes[n][:, :, a * P : (a + 1) * P].rearrange("p t r -> p r t"),
-                )
+        def group_h1(n, groups, engine):
+            if n not in h1_grouped:
+                h1_grouped[n] = hidden.tile([P, UNIT * PACK], BF16, name="h1_grouped", align_bytes=64)
+            for a in groups:
+                dst = h1_grouped[n][:, a * FEAT : (a + 1) * FEAT]
+                src = planes[n][:, :, a * P : (a + 1) * P]
+                if engine == "gpsimd":
+                    gpsimd_copy(dst.rearrange("p (r t) -> p r t", t=PACK), src.rearrange("p t r -> p r t"))
+                else:
+                    nc.vector.tensor_copy(
+                        out=dst.rearrange("p (c i t) -> p c t i", i=4, t=PACK),
+                        in_=src.rearrange("p t (c i) -> p c t i", i=4),
+                    )
 
         def quantise_h1(n, first, last):
             if first == 0:
@@ -241,62 +241,47 @@ def tile_declayerj_pa_t_kernel(tc, h_V, h_E, W1_w, W1_b, W2_w, W2_b, out):
                     hidden.tile([P, UNIT], U32, name="h1_codes", align_bytes=64),
                     hidden.tile([P, UNIT], U8, name="h1_scales", align_bytes=64),
                 )
-                banks_2[n] = {}
                 results[n] = result.tile([P, SUBS * FEAT], F32, name="z")
             codes, scales = h1_mx[n]
             cols = slice(first * P, last * P)
             quantise(codes[:, cols], scales[:, cols], h1_grouped[n][:, first * FEAT : last * FEAT])
 
-        def stage2_matmuls(n, first, last):
+        def stage2_matmul(n, a):
             codes, scales = h1_mx[n]
-            for a in range(first, last):
-                cols = slice(a * P, (a + 1) * P)
-                banks_2[n][a] = ps_2.tile([P, FEAT], F32, name="acc2")
-                mx_pass(banks_2[n][a][:], codes[:, cols], scales[:, cols], w2["codes"][:], w2["scales"][:], True, True)
+            cols = slice(a * P, (a + 1) * P)
+            banks_2[n, a] = ps_2.tile([P, FEAT], F32, name="acc2")
+            mx_pass(banks_2[n, a][:], codes[:, cols], scales[:, cols], w2["codes"][:], w2["scales"][:], True, True)
 
-        def stage2_bias(n, first, last):
-            for a in range(first, last):
-                nc.vector.tensor_tensor(
-                    out=results[n][:, a * FEAT : (a + 1) * FEAT], in0=banks_2[n][a][:], in1=b2_all[:], op=ADD
-                )
+        def stage2_bias(n, a):
+            nc.vector.tensor_tensor(
+                out=results[n][:, a * FEAT : (a + 1) * FEAT], in0=banks_2[n, a][:], in1=b2_all[:], op=ADD
+            )
 
         def stage2_gelu_and_store(n, first, last):
             cols = slice(first * FEAT, last * FEAT)
             nc.scalar.activation(out=results[n][:, cols], in_=results[n][:, cols], func=GELU)
             nc.sync.dma_start(out=out_units[n // BLOCK_UNITS, n % BLOCK_UNITS][:, cols], in_=results[n][:, cols])
 
+        V_COPY, S_COPY = nc.vector.tensor_copy, nc.scalar.copy
         group_nodes()
         transpose_edges(0)
         quantise(node_codes[:], node_scales[:], node_grouped[:])
-        group_edges(0, 0, nc.scalar.copy)
+        group_edges(0, 0, S_COPY)
         group_edges(0, 1)
         repeat_nodes(0)
         quantise_edges(0)
         for half, raw in (("nodes", w1v_raw), ("edges", w1e_raw)):
             for t in (0, 1):
-                group_w1(half, raw, t, nc.vector.tensor_copy)
+                group_w1(half, raw, t, V_COPY)
             for t in (2, 3):
-                group_w1(half, raw, t, nc.scalar.copy)
+                group_w1(half, raw, t, S_COPY)
             for t in range(PACK):
                 quantise_w1(half, t)
         transpose_edges(1)
-        group_edges(1, 0, nc.scalar.copy)
-        group_edges(1, 1, nc.scalar.copy)
-        stage1_matmuls(0, range(3))
-        transpose_edges(2)
-        stage1_matmuls(0, [3])
+        group_edges(1, 0, S_COPY)
+        group_edges(1, 1, S_COPY)
+        stage1_matmuls(0, [0])
         quantise_edges(1)
-        group_w2()
-        group_edges(2, 0)
-        group_edges(2, 1)
-        stage1_gelu(0)
-        stage1_matmuls(1, range(2))
-        transpose_edges(3)
-        stage1_matmuls(1, range(2, 4))
-        quantise_w2()
-        quantise_edges(2)
-        group_h1(0)
-        group_edges(3, 0)
 
         def in_range(n):
             return 0 <= n < UNITS
@@ -304,41 +289,56 @@ def tile_declayerj_pa_t_kernel(tc, h_V, h_E, W1_w, W1_b, W2_w, W2_b, out):
         def whole(n):
             return 0 <= n < UNITS - 1
 
-        for i in range(1, UNITS + 1):
-            if in_range(i):
-                stage1_gelu(i)
-            if whole(i - 1):
-                quantise_h1(i - 1, 0, SUBS)
-            if in_range(i + 2):
-                if i == 1:
-                    group_edges(i + 2, 1)
-                quantise_edges(i + 2)
-            if in_range(i + 1) and i == 1:
-                stage1_matmuls(i + 1)
-                transpose_edges(i + 3)
-            if whole(i - 1):
-                stage2_matmuls(i - 1, 0, SUBS)
-            if in_range(i + 3):
-                group_edges(i + 3, 0)
-            if whole(i - 1):
-                stage2_bias(i - 1, 0, SUBS)
-            if in_range(i + 3):
-                group_edges(i + 3, 1)
-            if i == 1:
-                repeat_nodes(1)
-            if in_range(i):
-                group_h1(i)
-            if whole(i - 2):
-                stage2_gelu_and_store(i - 2, 0, SUBS)
-            if in_range(i + 1) and i > 1:
-                stage1_matmuls(i + 1)
-            if in_range(i + 4):
-                transpose_edges(i + 4)
+        for i in range(UNITS + 1):
+            for a in range(SUBS):
+                if a < 3 and whole(i - 2):
+                    stage2_matmul(i - 2, a)
+                if a == 2 and whole(i - 2):
+                    stage2_matmul(i - 2, 3)
+                if a == 3 and in_range(i + 3):
+                    transpose_edges(i + 3)
+                if in_range(i if a < 3 else i + 1):
+                    stage1_matmuls(i if a < 3 else i + 1, [(a + 1) % 4])
+                if in_range(i):
+                    stage1_gelu(i, a)
+                if i == 0 and a == 0:
+                    transpose_edges(2)
+                if a == 0 and i == UNITS:
+                    group_h1(i - 1, (2, 3), "gpsimd")
+                    group_h1(i - 1, (0,), "vector")
+                if a == 0 and whole(i - 1):
+                    group_h1(i - 1, range(SUBS), "vector" if i == 1 else "gpsimd")
+                if i == 0 and a == 0:
+                    group_w2()
+                    quantise_w2()
+                if i == 0 and a == 3:
+                    repeat_nodes(1)
+                if a < 2 and in_range(i + 2):
+                    group_edges(i + 2, a, S_COPY if i < 3 or (a == 1 and i % 4 == 0) else V_COPY)
+                if whole(i - 2):
+                    stage2_bias(i - 2, a)
+                if i == UNITS and a == 1:
+                    group_h1(i - 1, (1,), "vector")
+                if i == UNITS and a == 2:
+                    quantise_h1(UNITS - 1, 0, 1)
+                if i == UNITS and a == 3:
+                    stage2_matmul(UNITS - 1, 0)
+                if a == 3:
+                    if whole(i - 1):
+                        quantise_h1(i - 1, 0, SUBS)
+                    if in_range(i + 2):
+                        quantise_edges(i + 2)
+                if a == 0 and whole(i - 3):
+                    stage2_gelu_and_store(i - 3, 2, 4)
+                if a == 2 and whole(i - 2):
+                    stage2_gelu_and_store(i - 2, 0, 2)
 
+        stage2_gelu_and_store(UNITS - 2, 2, 4)
+        n = UNITS - 1
         for a in range(SUBS + 1):
-            if a < SUBS:
-                quantise_h1(UNITS - 1, a, a + 1)
-                stage2_matmuls(UNITS - 1, a, a + 1)
+            if 0 < a < SUBS:
+                quantise_h1(n, a, a + 1)
+                stage2_matmul(n, a)
             if a > 0:
-                stage2_bias(UNITS - 1, a - 1, a)
-                stage2_gelu_and_store(UNITS - 1, a - 1, a)
+                stage2_bias(n, a - 1)
+                stage2_gelu_and_store(n, a - 1, a)

@@ -98,10 +98,11 @@ def tile_declayerj_pa_t_kernel(tc, h_V, h_E, W1_w, W1_b, W2_w, W2_b, out):
         nc.sync.dma_start(
             out=w2_raw[:].rearrange("p j n -> p (j n)"), in_=W2_w.rearrange("(p j) n -> p (j n)", j=PACK)
         )
-        load_unit(2)
+        for n in range(2, 5):
+            load_unit(n)
         b2_all = consts.tile([P, FEAT], BF16)
         nc.sync.dma_start(out=b2_all[:], in_=W2_b.partition_broadcast(P))
-        for n in range(3, UNITS):
+        for n in range(5, UNITS):
             load_unit(n)
 
         ident = consts.tile([P, P], F32)

@@ -43,7 +43,7 @@ def tile_declayerj_pa_t_kernel(tc, h_V, h_E, W1_w, W1_b, W2_w, W2_b, out):
         prep = ctx.enter_context(tc.tile_pool(name="prep", bufs=3))
         edges_in = ctx.enter_context(tc.tile_pool(name="edges_in", bufs=UNITS))
         node_pool = ctx.enter_context(tc.tile_pool(name="node_pool", bufs=2))
-        front = ctx.enter_context(tc.tile_pool(name="front", bufs=4))
+        pairs = ctx.enter_context(tc.tile_pool(name="pairs", bufs=4))
         hidden = ctx.enter_context(tc.tile_pool(name="hidden", bufs=3))
         result = ctx.enter_context(tc.tile_pool(name="result", bufs=4))
         ps_t = ctx.enter_context(tc.psum_pool(name="ps_t", bufs=2))
@@ -177,9 +177,8 @@ def tile_declayerj_pa_t_kernel(tc, h_V, h_E, W1_w, W1_b, W2_w, W2_b, out):
             )
             node_operands[g] = (codes, scales)
 
-        banks_t, edge_grouped, edge_mx, banks_1, planes, h1_grouped, h1_mx, banks_2, results = (
-            {}, {}, {}, {}, {}, {}, {}, {}, {},
-        )
+        banks_t, pair_tiles, banks_1, planes, banks_2, results = {}, {}, {}, {}, {}, {}
+
         def transpose_edges(n):
             words = edge_tiles[n][:].bitcast(F32)
             banks_t[n] = []
@@ -191,20 +190,26 @@ def tile_declayerj_pa_t_kernel(tc, h_V, h_E, W1_w, W1_b, W2_w, W2_b, out):
                         nc.tensor.transpose(bank[:, a, u, :], words[:, first : first + P], ident[:])
                 banks_t[n].append(bank)
 
+        def pair_of(m):
+            if m not in pair_tiles:
+                pair_tiles[m] = (
+                    pairs.tile([P, 2 * UNIT * PACK], BF16, name="pair_grouped", align_bytes=64),
+                    pairs.tile([P, 2 * UNIT], U32, name="pair_codes", align_bytes=64),
+                    pairs.tile([P, 2 * UNIT], U8, name="pair_scales", align_bytes=64),
+                )
+            return pair_tiles[m]
+
         def group_edges(n, b, copy=nc.vector.tensor_copy):
-            if b == 0:
-                edge_grouped[n] = front.tile([P, UNIT * PACK], BF16, name="edge_grouped", align_bytes=64)
-            grouped_words = edge_grouped[n][:].bitcast(F32).rearrange("p (a r u) -> p a r u", a=SUBS, u=2)
+            grouped = pair_of(n - 3)[0][:, UNIT * PACK :]
+            grouped_words = grouped.bitcast(F32).rearrange("p (a r u) -> p a r u", a=SUBS, u=2)
             copy(out=grouped_words[:, 2 * b : 2 * b + 2], in_=banks_t[n][b][:].rearrange("p a u r -> p a r u"))
 
-        def quantise_edges(n):
-            codes = front.tile([P, UNIT], U32, name="edge_codes", align_bytes=64)
-            scales = front.tile([P, UNIT], U8, name="edge_scales", align_bytes=64)
-            quantise(codes[:], scales[:], edge_grouped[n][:])
-            edge_mx[n] = (codes, scales)
+        def quantise_pair(m, first, last):
+            grouped, codes, scales = pair_of(m)
+            quantise(codes[:, first:last], scales[:, first:last], grouped[:, first * PACK : last * PACK])
 
         def stage1_matmuls(n, tiles=range(PACK)):
-            e_codes, e_scales = edge_mx[n]
+            e_codes, e_scales = [tile[:, UNIT:] for tile in pair_of(n - 3)[1:]]
             v_codes, v_scales = node_operands[n // BLOCK_UNITS]
             w1e_codes, w1e_scales = w1["edges"][1:]
             w1v_codes, w1v_scales = w1["nodes"][1:]
@@ -212,7 +217,7 @@ def tile_declayerj_pa_t_kernel(tc, h_V, h_E, W1_w, W1_b, W2_w, W2_b, out):
                 cols = slice(t * P, (t + 1) * P)
                 acc = ps_1.tile([P, UNIT], F32, name="acc1")
                 mx_pass(acc[:], w1v_codes[:, cols], w1v_scales[:, cols], v_codes[:], v_scales[:], True, False)
-                mx_pass(acc[:], w1e_codes[:, cols], w1e_scales[:, cols], e_codes[:], e_scales[:], False, True)
+                mx_pass(acc[:], w1e_codes[:, cols], w1e_scales[:, cols], e_codes, e_scales, False, True)
                 banks_1[n, t] = acc
 
         def stage1_gelu(n, t):
@@ -223,10 +228,8 @@ def tile_declayerj_pa_t_kernel(tc, h_V, h_E, W1_w, W1_b, W2_w, W2_b, out):
             )
 
         def group_h1(n, groups, engine):
-            if n not in h1_grouped:
-                h1_grouped[n] = hidden.tile([P, UNIT * PACK], BF16, name="h1_grouped", align_bytes=64)
             for a in groups:
-                dst = h1_grouped[n][:, a * FEAT : (a + 1) * FEAT]
+                dst = pair_of(n)[0][:, a * FEAT : (a + 1) * FEAT]
                 src = planes[n][:, :, a * P : (a + 1) * P]
                 if engine == "gpsimd":
                     gpsimd_copy(dst.rearrange("p (r t) -> p r t", t=PACK), src.rearrange("p t r -> p r t"))
@@ -236,19 +239,10 @@ def tile_declayerj_pa_t_kernel(tc, h_V, h_E, W1_w, W1_b, W2_w, W2_b, out):
                         in_=src.rearrange("p t (c i) -> p c t i", i=4),
                     )
 
-        def quantise_h1(n, first, last):
-            if first == 0:
-                h1_mx[n] = (
-                    hidden.tile([P, UNIT], U32, name="h1_codes", align_bytes=64),
-                    hidden.tile([P, UNIT], U8, name="h1_scales", align_bytes=64),
-                )
-                results[n] = result.tile([P, SUBS * FEAT], F32, name="z")
-            codes, scales = h1_mx[n]
-            cols = slice(first * P, last * P)
-            quantise(codes[:, cols], scales[:, cols], h1_grouped[n][:, first * FEAT : last * FEAT])
-
         def stage2_matmul(n, a):
-            codes, scales = h1_mx[n]
+            if a == 0:
+                results[n] = result.tile([P, SUBS * FEAT], F32, name="z")
+            codes, scales = pair_of(n)[1:]
             cols = slice(a * P, (a + 1) * P)
             banks_2[n, a] = ps_2.tile([P, FEAT], F32, name="acc2")
             mx_pass(banks_2[n, a][:], codes[:, cols], scales[:, cols], w2["codes"][:], w2["scales"][:], True, True)
@@ -267,22 +261,46 @@ def tile_declayerj_pa_t_kernel(tc, h_V, h_E, W1_w, W1_b, W2_w, W2_b, out):
         group_nodes()
         transpose_edges(0)
         quantise(node_codes[:], node_scales[:], node_grouped[:])
-        group_edges(0, 0, S_COPY)
-        group_edges(0, 1)
         repeat_nodes(0)
-        quantise_edges(0)
-        for half, raw in (("nodes", w1v_raw), ("edges", w1e_raw)):
-            for t in (0, 1):
-                group_w1(half, raw, t, V_COPY)
-            for t in (2, 3):
-                group_w1(half, raw, t, S_COPY)
-            for t in range(PACK):
-                quantise_w1(half, t)
+        group_edges(0, 0, S_COPY)
+        group_edges(0, 1, S_COPY)
+        group_w1("nodes", w1v_raw, 0, V_COPY)
+        group_w1("nodes", w1v_raw, 1, S_COPY)
+        quantise_w1("nodes", 0)
+        quantise_pair(0 - 3, UNIT, 2 * UNIT)
+        group_w1("edges", w1e_raw, 0, V_COPY)
+        group_w1("edges", w1e_raw, 1, S_COPY)
+        quantise_w1("edges", 0)
+        stage1_matmuls(0, [0])
+        quantise_w1("nodes", 1)
+        group_w1("nodes", w1v_raw, 2, V_COPY)
+        quantise_w1("edges", 1)
+        stage1_matmuls(0, [1])
+        group_w1("edges", w1e_raw, 2, V_COPY)
+        quantise_w1("nodes", 2)
+        quantise_w1("edges", 2)
+        group_w1("nodes", w1v_raw, 3, S_COPY)
+        group_w1("edges", w1e_raw, 3, S_COPY)
+        quantise_w1("nodes", 3)
+        quantise_w1("edges", 3)
+        stage1_gelu(0, 0)
+        stage1_gelu(0, 1)
         transpose_edges(1)
         group_edges(1, 0, S_COPY)
-        group_edges(1, 1, S_COPY)
-        stage1_matmuls(0, [0])
-        quantise_edges(1)
+        group_edges(1, 1)
+        stage1_matmuls(0, [2, 3])
+        stage1_gelu(0, 2)
+        stage1_gelu(0, 3)
+        quantise_pair(1 - 3, UNIT, 2 * UNIT)
+        transpose_edges(2)
+        group_w2()
+        group_edges(2, 0, S_COPY)
+        group_edges(2, 1, S_COPY)
+        stage1_matmuls(1, [0])
+        quantise_w2()
+        quantise_pair(2 - 3, UNIT, 2 * UNIT)
+        transpose_edges(3)
+        repeat_nodes(1)
 
         def in_range(n):
             return 0 <= n < UNITS
@@ -290,56 +308,118 @@ def tile_declayerj_pa_t_kernel(tc, h_V, h_E, W1_w, W1_b, W2_w, W2_b, out):
         def whole(n):
             return 0 <= n < UNITS - 1
 
-        for i in range(UNITS + 1):
-            for a in range(SUBS):
-                if a < 3 and whole(i - 2):
-                    stage2_matmul(i - 2, a)
-                if a == 2 and whole(i - 2):
-                    stage2_matmul(i - 2, 3)
-                if a == 3 and in_range(i + 3):
-                    transpose_edges(i + 3)
-                if in_range(i if a < 3 else i + 1):
-                    stage1_matmuls(i if a < 3 else i + 1, [(a + 1) % 4])
-                if in_range(i):
-                    stage1_gelu(i, a)
-                if i == 0 and a == 0:
-                    transpose_edges(2)
-                if a == 0 and i == UNITS:
-                    group_h1(i - 1, (2, 3), "gpsimd")
-                    group_h1(i - 1, (0,), "vector")
-                if a == 0 and whole(i - 1):
-                    group_h1(i - 1, range(SUBS), "vector" if i == 1 else "gpsimd")
-                if i == 0 and a == 0:
-                    group_w2()
-                    quantise_w2()
-                if i == 0 and a == 3:
-                    repeat_nodes(1)
-                if a < 2 and in_range(i + 2):
-                    group_edges(i + 2, a, S_COPY if i < 3 or (a == 1 and i % 4 == 0) else V_COPY)
-                if whole(i - 2):
-                    stage2_bias(i - 2, a)
-                if i == UNITS and a == 1:
-                    group_h1(i - 1, (1,), "vector")
-                if i == UNITS and a == 2:
-                    quantise_h1(UNITS - 1, 0, 1)
-                if i == UNITS and a == 3:
-                    stage2_matmul(UNITS - 1, 0)
-                if a == 3:
-                    if whole(i - 1):
-                        quantise_h1(i - 1, 0, SUBS)
-                    if in_range(i + 2):
-                        quantise_edges(i + 2)
-                if a == 0 and whole(i - 3):
-                    stage2_gelu_and_store(i - 3, 2, 4)
-                if a == 2 and whole(i - 2):
-                    stage2_gelu_and_store(i - 2, 0, 2)
+        for i in range(1, 15):
+            if in_range(i):
+                stage1_matmuls(i, [1])
+            if whole(i - 2):
+                stage2_matmul(i - 2, 0)
+            if whole(i - 2):
+                stage2_matmul(i - 2, 1)
+            if in_range(i):
+                stage1_gelu(i, 0)
+            if i >= UNITS - 1:
+                group_h1(i - 1, (2, 3), "gpsimd")
+            if i >= UNITS - 1:
+                group_h1(i - 1, (0,), "vector")
+            if 1 < i < UNITS - 1:
+                group_h1(i - 1, range(SUBS), "gpsimd")
+            if i == 1:
+                group_h1(i - 1, range(SUBS), "vector")
+            if in_range(i + 2) and not (i < 3):
+                group_edges(i + 2, 0)
+            if in_range(i + 2) and (i < 3):
+                group_edges(i + 2, 0, S_COPY)
+            if in_range(i + 2) and not (i < 3 or i % 5 == 0):
+                group_edges(i + 2, 1)
+            if whole(i - 2):
+                stage2_bias(i - 2, 0)
+            if whole(i - 3):
+                stage2_gelu_and_store(i - 3, 2, 4)
+            if in_range(i):
+                stage1_matmuls(i, [2])
+            if whole(i - 2):
+                stage2_matmul(i - 2, 2)
+            if in_range(i):
+                stage1_gelu(i, 1)
+            if in_range(i + 2) and (i < 3 or i % 5 == 0):
+                group_edges(i + 2, 1, S_COPY)
+            if whole(i - 2):
+                stage2_bias(i - 2, 1)
+            if i >= UNITS - 1:
+                group_h1(i - 1, (1,), "vector")
+            if in_range(i):
+                stage1_matmuls(i, [3])
+            if whole(i - 2):
+                stage2_matmul(i - 2, 3)
+            if in_range(i + 3):
+                transpose_edges(i + 3)
+            if in_range(i):
+                stage1_gelu(i, 2)
+            if whole(i - 2):
+                stage2_bias(i - 2, 2)
+            if i == UNITS:
+                quantise_pair(i - 1, 0, 128)
+            if whole(i - 2):
+                stage2_gelu_and_store(i - 2, 0, 2)
+            if in_range(i + 1):
+                stage1_matmuls(i + 1, [0])
+            if in_range(i):
+                stage1_gelu(i, 3)
+            if whole(i - 2):
+                stage2_bias(i - 2, 3)
+            if i == UNITS:
+                stage2_matmul(i - 1, 0)
+            if 0 < i < UNITS:
+                quantise_pair(i - 1, 0, 2 * UNIT if in_range(i + 2) else UNIT)
 
-        stage2_gelu_and_store(UNITS - 2, 2, 4)
-        n = UNITS - 1
-        for a in range(SUBS + 1):
-            if 0 < a < SUBS:
-                quantise_h1(n, a, a + 1)
-                stage2_matmul(n, a)
-            if a > 0:
-                stage2_bias(n, a - 1)
-                stage2_gelu_and_store(n, a - 1, a)
+        stage1_matmuls(15, [1])
+        stage2_matmul(13, 0)
+        stage2_matmul(13, 1)
+        stage1_gelu(15, 0)
+        group_h1(14, (2,), "gpsimd")
+        group_h1(14, (3,), "gpsimd")
+        group_h1(14, (0,), "vector")
+        stage2_bias(13, 0)
+        stage2_gelu_and_store(12, 2, 4)
+        stage1_matmuls(15, [2])
+        stage2_matmul(13, 2)
+        stage1_gelu(15, 1)
+        stage2_bias(13, 1)
+        group_h1(14, (1,), "vector")
+        stage1_matmuls(15, [3])
+        stage2_matmul(13, 3)
+        stage1_gelu(15, 2)
+        quantise_pair(14, 0, 512)
+        stage2_bias(13, 2)
+        stage2_gelu_and_store(13, 0, 2)
+        stage1_gelu(15, 3)
+        stage2_bias(13, 3)
+        stage2_matmul(14, 0)
+        stage2_matmul(14, 1)
+        group_h1(15, (0,), "gpsimd")
+        group_h1(15, (1,), "gpsimd")
+        group_h1(15, (2,), "gpsimd")
+        stage2_bias(14, 0)
+        stage2_gelu_and_store(13, 2, 4)
+        stage2_matmul(14, 2)
+        stage2_bias(14, 1)
+        stage2_gelu_and_store(14, 0, 2)
+        stage2_matmul(14, 3)
+        stage2_bias(14, 2)
+        stage2_bias(14, 3)
+        stage2_gelu_and_store(14, 2, 4)
+        group_h1(15, (3,), "vector")
+        quantise_pair(15, 0, 256)
+        stage2_matmul(15, 0)
+        stage2_matmul(15, 1)
+        quantise_pair(15, 256, 512)
+        stage2_bias(15, 0)
+        stage2_gelu_and_store(15, 0, 1)
+        stage2_matmul(15, 2)
+        stage2_bias(15, 1)
+        stage2_gelu_and_store(15, 1, 2)
+        stage2_matmul(15, 3)
+        stage2_bias(15, 2)
+        stage2_gelu_and_store(15, 2, 3)
+        stage2_bias(15, 3)
+        stage2_gelu_and_store(15, 3, 4)

@@ -329,7 +329,7 @@ def tile_declayerj_pa_t_kernel(tc, h_V, h_E, W1_w, W1_b, W2_w, W2_b, out):
                 group_edges(i + 2, 0)
             if in_range(i + 2) and (i < 3):
                 group_edges(i + 2, 0, S_COPY)
-            if in_range(i + 2) and not (i < 3 or i % 5 == 0):
+            if in_range(i + 2) and not (i < 3):
                 group_edges(i + 2, 1)
             if whole(i - 2):
                 stage2_bias(i - 2, 0)
@@ -341,7 +341,7 @@ def tile_declayerj_pa_t_kernel(tc, h_V, h_E, W1_w, W1_b, W2_w, W2_b, out):
                 stage2_matmul(i - 2, 2)
             if in_range(i):
                 stage1_gelu(i, 1)
-            if in_range(i + 2) and (i < 3 or i % 5 == 0):
+            if in_range(i + 2) and (i < 3):
                 group_edges(i + 2, 1, S_COPY)
             if whole(i - 2):
                 stage2_bias(i - 2, 1)

@@ -228,9 +228,10 @@ def tile_declayerj_pa_t_kernel(tc, h_V, h_E, W1_w, W1_b, W2_w, W2_b, out):
             )
 
         def group_h1(n, groups, engine):
-            for a in groups:
-                dst = pair_of(n)[0][:, a * FEAT : (a + 1) * FEAT]
-                src = planes[n][:, :, a * P : (a + 1) * P]
+            step = 2 if engine == "gpsimd" else 1
+            for a in groups[::step]:
+                dst = pair_of(n)[0][:, a * FEAT : (a + min(step, len(groups))) * FEAT]
+                src = planes[n][:, :, a * P : (a + min(step, len(groups))) * P]
                 if engine == "gpsimd":
                     gpsimd_copy(dst.rearrange("p (r t) -> p r t", t=PACK), src.rearrange("p t r -> p r t"))
                 else:

@@ -227,18 +227,16 @@ def tile_declayerj_pa_t_kernel(tc, h_V, h_E, W1_w, W1_b, W2_w, W2_b, out):
                 out=planes[n][:, t, :], in_=banks_1[n, t][:], func=GELU, bias=b1_bf[:, t : t + 1], scale=1.0
             )
 
-        def group_h1(n, groups, engine):
-            step = 2 if engine == "gpsimd" else 1
-            for a in groups[::step]:
-                dst = pair_of(n)[0][:, a * FEAT : (a + min(step, len(groups))) * FEAT]
-                src = planes[n][:, :, a * P : (a + min(step, len(groups))) * P]
-                if engine == "gpsimd":
-                    gpsimd_copy(dst.rearrange("p (r t) -> p r t", t=PACK), src.rearrange("p t r -> p r t"))
-                else:
-                    nc.vector.tensor_copy(
-                        out=dst.rearrange("p (c i t) -> p c t i", i=4, t=PACK),
-                        in_=src.rearrange("p t (c i) -> p c t i", i=4),
-                    )
+        def group_h1(n, first, last, engine):
+            dst = pair_of(n)[0][:, first * FEAT : last * FEAT]
+            src = planes[n][:, :, first * P : last * P]
+            if engine == "gpsimd":
+                gpsimd_copy(dst.rearrange("p (r t) -> p r t", t=PACK), src.rearrange("p t r -> p r t"))
+            else:
+                nc.vector.tensor_copy(
+                    out=dst.rearrange("p (c i t) -> p c t i", i=4, t=PACK),
+                    in_=src.rearrange("p t (c i) -> p c t i", i=4),
+                )
 
         def stage2_matmul(n, a):
             if a == 0:
@@ -318,14 +316,10 @@ def tile_declayerj_pa_t_kernel(tc, h_V, h_E, W1_w, W1_b, W2_w, W2_b, out):
                 stage2_matmul(i - 2, 1)
             if in_range(i):
                 stage1_gelu(i, 0)
-            if i >= UNITS - 1:
-                group_h1(i - 1, (2, 3), "gpsimd")
-            if i >= UNITS - 1:
-                group_h1(i - 1, (0,), "vector")
             if 1 < i < UNITS - 1:
-                group_h1(i - 1, range(SUBS), "gpsimd")
+                group_h1(i - 1, 0, SUBS, "gpsimd")
             if i == 1:
-                group_h1(i - 1, range(SUBS), "vector")
+                group_h1(i - 1, 0, SUBS, "vector")
             if in_range(i + 2) and not (i < 3):
                 group_edges(i + 2, 0)
             if in_range(i + 2) and (i < 3):
@@ -346,8 +340,6 @@ def tile_declayerj_pa_t_kernel(tc, h_V, h_E, W1_w, W1_b, W2_w, W2_b, out):
                 group_edges(i + 2, 1, S_COPY)
             if whole(i - 2):
                 stage2_bias(i - 2, 1)
-            if i >= UNITS - 1:
-                group_h1(i - 1, (1,), "vector")
             if in_range(i):
                 stage1_matmuls(i, [3])
             if whole(i - 2):
@@ -358,8 +350,6 @@ def tile_declayerj_pa_t_kernel(tc, h_V, h_E, W1_w, W1_b, W2_w, W2_b, out):
                 stage1_gelu(i, 2)
             if whole(i - 2):
                 stage2_bias(i - 2, 2)
-            if i == UNITS:
-                quantise_pair(i - 1, 0, 128)
             if whole(i - 2):
                 stage2_gelu_and_store(i - 2, 0, 2)
             if in_range(i + 1):
@@ -368,8 +358,6 @@ def tile_declayerj_pa_t_kernel(tc, h_V, h_E, W1_w, W1_b, W2_w, W2_b, out):
                 stage1_gelu(i, 3)
             if whole(i - 2):
                 stage2_bias(i - 2, 3)
-            if i == UNITS:
-                stage2_matmul(i - 1, 0)
             if 0 < i < UNITS:
                 quantise_pair(i - 1, 0, 2 * UNIT if in_range(i + 2) else UNIT)
 
@@ -377,16 +365,14 @@ def tile_declayerj_pa_t_kernel(tc, h_V, h_E, W1_w, W1_b, W2_w, W2_b, out):
         stage2_matmul(13, 0)
         stage2_matmul(13, 1)
         stage1_gelu(15, 0)
-        group_h1(14, (2,), "gpsimd")
-        group_h1(14, (3,), "gpsimd")
-        group_h1(14, (0,), "vector")
+        group_h1(14, 2, 4, "gpsimd")
+        group_h1(14, 0, 2, "vector")
         stage2_bias(13, 0)
         stage2_gelu_and_store(12, 2, 4)
         stage1_matmuls(15, [2])
         stage2_matmul(13, 2)
         stage1_gelu(15, 1)
         stage2_bias(13, 1)
-        group_h1(14, (1,), "vector")
         stage1_matmuls(15, [3])
         stage2_matmul(13, 3)
         stage1_gelu(15, 2)
@@ -397,9 +383,7 @@ def tile_declayerj_pa_t_kernel(tc, h_V, h_E, W1_w, W1_b, W2_w, W2_b, out):
         stage2_bias(13, 3)
         stage2_matmul(14, 0)
         stage2_matmul(14, 1)
-        group_h1(15, (0,), "gpsimd")
-        group_h1(15, (1,), "gpsimd")
-        group_h1(15, (2,), "gpsimd")
+        group_h1(15, 0, 3, "gpsimd")
         stage2_bias(14, 0)
         stage2_gelu_and_store(13, 2, 4)
         stage2_matmul(14, 2)
@@ -409,7 +393,7 @@ def tile_declayerj_pa_t_kernel(tc, h_V, h_E, W1_w, W1_b, W2_w, W2_b, out):
         stage2_bias(14, 2)
         stage2_bias(14, 3)
         stage2_gelu_and_store(14, 2, 4)
-        group_h1(15, (3,), "vector")
+        group_h1(15, 3, 4, "vector")
         quantise_pair(15, 0, 256)
         stage2_matmul(15, 0)
         stage2_matmul(15, 1)

@@ -82,8 +82,9 @@ def tile_declayerj_pa_t_kernel(tc, h_V, h_E, W1_w, W1_b, W2_w, W2_b, out):
             edge_tiles[n] = edges_in.tile([P, SUBS * FEAT], BF16, name="edge_rows")
             nc.sync.dma_start(out=edge_tiles[n][:], in_=edge_units[n // BLOCK_UNITS, n % BLOCK_UNITS])
 
-        b1_bf = consts.tile([P, PACK], BF16)
-        nc.scalar.dma_start(out=b1_bf[:], in_=W1_b.rearrange("(p t) -> p t", t=PACK))
+        b1_rows = consts.tile([P, P], BF16)
+        nc.vector.memset(b1_rows[:], 0.0)
+        nc.scalar.dma_start(out=b1_rows[0:PACK, :], in_=W1_b.rearrange("(t p) -> t p", t=PACK))
 
         node_rows = consts.tile([P, 2 * FEAT], BF16)
         nc.sync.dma_start(
@@ -96,7 +97,7 @@ def tile_declayerj_pa_t_kernel(tc, h_V, h_E, W1_w, W1_b, W2_w, W2_b, out):
         load_unit(1)
         w2_raw = prep.tile([P, PACK, FEAT], BF16, name="w_raw")
         nc.sync.dma_start(
-            out=w2_raw[:].rearrange("p j n -> p (j n)"), in_=W2_w.rearrange("(p j) n -> p (j n)", j=PACK)
+            out=w2_raw[:], in_=W2_w.rearrange("(j p) n -> p j n", j=PACK)
         )
         for n in range(2, 5):
             load_unit(n)
@@ -111,6 +112,15 @@ def tile_declayerj_pa_t_kernel(tc, h_V, h_E, W1_w, W1_b, W2_w, W2_b, out):
         nc.vector.memset(warm[:], 0.0)
         nc.scalar.activation(out=warm[:, 1:2], in_=warm[:, 0:1], func=GELU)
 
+        b1 = consts.tile([P, PACK], F32)
+
+        def turn_b1():
+            unit = consts.tile([P, PACK], BF16)
+            nc.vector.tensor_copy(out=unit[:], in_=ident[:, 0:PACK])
+            bank = ps_2.tile([P, FEAT], F32, name="acc2")
+            nc.tensor.matmul(out=bank[:, 0:PACK], lhsT=b1_rows[:], rhs=unit[:], start=True, stop=True)
+            return bank
+
         w1 = {}
         for half in ("nodes", "edges"):
             w1[half] = (
@@ -122,7 +132,7 @@ def tile_declayerj_pa_t_kernel(tc, h_V, h_E, W1_w, W1_b, W2_w, W2_b, out):
         def group_w1(half, raw, t, copy):
             copy(
                 out=w1[half][0][:, t * FEAT : (t + 1) * FEAT].rearrange("q (p j) -> q p j", j=PACK),
-                in_=raw[:].rearrange("q j (p t) -> q t p j", t=PACK)[:, t],
+                in_=raw[:, :, t * P : (t + 1) * P].rearrange("q j p -> q p j"),
             )
 
         def quantise_w1(half, t):
@@ -224,7 +234,7 @@ def tile_declayerj_pa_t_kernel(tc, h_V, h_E, W1_w, W1_b, W2_w, W2_b, out):
             if t == 0:
                 planes[n] = hidden.tile([P, PACK, UNIT], BF16, name="h1_planes")
             nc.scalar.activation(
-                out=planes[n][:, t, :], in_=banks_1[n, t][:], func=GELU, bias=b1_bf[:, t : t + 1], scale=1.0
+                out=planes[n][:, t, :], in_=banks_1[n, t][:], func=GELU, bias=b1[:, t : t + 1], scale=1.0
             )
 
         def group_h1(n, first, last, engine):
@@ -259,6 +269,7 @@ def tile_declayerj_pa_t_kernel(tc, h_V, h_E, W1_w, W1_b, W2_w, W2_b, out):
         V_COPY, S_COPY = nc.vector.tensor_copy, nc.scalar.copy
         group_nodes()
         transpose_edges(0)
+        b1_bank = turn_b1()
         quantise(node_codes[:], node_scales[:], node_grouped[:])
         repeat_nodes(0)
         group_edges(0, 0, S_COPY)
@@ -271,6 +282,7 @@ def tile_declayerj_pa_t_kernel(tc, h_V, h_E, W1_w, W1_b, W2_w, W2_b, out):
         group_w1("edges", w1e_raw, 1, S_COPY)
         quantise_w1("edges", 0)
         stage1_matmuls(0, [0])
+        nc.vector.tensor_copy(out=b1[:], in_=b1_bank[:, 0:PACK])
         quantise_w1("nodes", 1)
         group_w1("nodes", w1v_raw, 2, V_COPY)
         quantise_w1("edges", 1)

@@ -280,26 +280,26 @@ def tile_declayerj_pa_t_kernel(tc, h_V, h_E, W1_w, W1_b, W2_w, W2_b, out):
         quantise_pair(0 - 3, UNIT, 2 * UNIT)
         group_w1("edges", w1e_raw, 0, V_COPY)
         group_w1("edges", w1e_raw, 1, S_COPY)
+        quantise_w1("nodes", 1)
         quantise_w1("edges", 0)
         stage1_matmuls(0, [0])
         nc.vector.tensor_copy(out=b1[:], in_=b1_bank[:, 0:PACK])
-        quantise_w1("nodes", 1)
         group_w1("nodes", w1v_raw, 2, V_COPY)
         quantise_w1("edges", 1)
         stage1_matmuls(0, [1])
         group_w1("edges", w1e_raw, 2, V_COPY)
         quantise_w1("nodes", 2)
-        quantise_w1("edges", 2)
         group_w1("nodes", w1v_raw, 3, S_COPY)
         group_w1("edges", w1e_raw, 3, S_COPY)
         quantise_w1("nodes", 3)
+        quantise_w1("edges", 2)
         quantise_w1("edges", 3)
         stage1_gelu(0, 0)
         stage1_gelu(0, 1)
         transpose_edges(1)
         group_edges(1, 0, S_COPY)
         group_edges(1, 1)
-        stage1_matmuls(0, [2, 3])
+        stage1_matmuls(0, [2,3])
         stage1_gelu(0, 2)
         stage1_gelu(0, 3)
         quantise_pair(1 - 3, UNIT, 2 * UNIT)
@@ -312,6 +312,19 @@ def tile_declayerj_pa_t_kernel(tc, h_V, h_E, W1_w, W1_b, W2_w, W2_b, out):
         quantise_pair(2 - 3, UNIT, 2 * UNIT)
         transpose_edges(3)
         repeat_nodes(1)
+        stage1_matmuls(1, [1])
+        stage1_gelu(1, 0)
+        group_h1(0, 0, SUBS, "vector")
+        group_edges(3, 0, S_COPY)
+        stage1_matmuls(1, [2])
+        stage1_gelu(1, 1)
+        group_edges(3, 1, S_COPY)
+        stage1_matmuls(1, [3])
+        transpose_edges(4)
+        stage1_gelu(1, 2)
+        stage1_matmuls(2, [0])
+        stage1_gelu(1, 3)
+        quantise_pair(0, 0, 2 * UNIT)
 
         def in_range(n):
             return 0 <= n < UNITS
@@ -319,7 +332,7 @@ def tile_declayerj_pa_t_kernel(tc, h_V, h_E, W1_w, W1_b, W2_w, W2_b, out):
         def whole(n):
             return 0 <= n < UNITS - 1
 
-        for i in range(1, 15):
+        for i in range(2, 15):
             if in_range(i):
                 stage1_matmuls(i, [1])
             if whole(i - 2):
@@ -330,8 +343,6 @@ def tile_declayerj_pa_t_kernel(tc, h_V, h_E, W1_w, W1_b, W2_w, W2_b, out):
                 stage1_gelu(i, 0)
             if 1 < i < UNITS - 1:
                 group_h1(i - 1, 0, SUBS, "gpsimd")
-            if i == 1:
-                group_h1(i - 1, 0, SUBS, "vector")
             if in_range(i + 2) and not (i < 3):
                 group_edges(i + 2, 0)
             if in_range(i + 2) and (i < 3):
@@ -352,10 +363,10 @@ def tile_declayerj_pa_t_kernel(tc, h_V, h_E, W1_w, W1_b, W2_w, W2_b, out):
                 group_edges(i + 2, 1, S_COPY)
             if whole(i - 2):
                 stage2_bias(i - 2, 1)
-            if in_range(i):
-                stage1_matmuls(i, [3])
             if whole(i - 2):
                 stage2_matmul(i - 2, 3)
+            if in_range(i):
+                stage1_matmuls(i, [3])
             if in_range(i + 3):
                 transpose_edges(i + 3)
             if in_range(i):
@@ -370,32 +381,35 @@ def tile_declayerj_pa_t_kernel(tc, h_V, h_E, W1_w, W1_b, W2_w, W2_b, out):
                 stage1_gelu(i, 3)
             if whole(i - 2):
                 stage2_bias(i - 2, 3)
-            if 0 < i < UNITS:
+            if 0 < i < UNITS and i != 13:
                 quantise_pair(i - 1, 0, 2 * UNIT if in_range(i + 2) else UNIT)
+            if i == 13:
+                quantise_pair(i - 1, 0, UNIT)
+                quantise_pair(i - 1, UNIT, 2 * UNIT)
 
         stage1_matmuls(15, [1])
         stage2_matmul(13, 0)
         stage2_matmul(13, 1)
         stage1_gelu(15, 0)
-        group_h1(14, 2, 4, "gpsimd")
         group_h1(14, 0, 2, "vector")
+        group_h1(14, 2, 4, "gpsimd")
         stage2_bias(13, 0)
+        stage2_bias(13, 1)
         stage2_gelu_and_store(12, 2, 4)
         stage1_matmuls(15, [2])
         stage2_matmul(13, 2)
         stage1_gelu(15, 1)
-        stage2_bias(13, 1)
         stage1_matmuls(15, [3])
         stage2_matmul(13, 3)
         stage1_gelu(15, 2)
-        quantise_pair(14, 0, 512)
         stage2_bias(13, 2)
+        quantise_pair(14, 0, 512)
         stage2_gelu_and_store(13, 0, 2)
-        stage1_gelu(15, 3)
         stage2_bias(13, 3)
+        stage1_gelu(15, 3)
         stage2_matmul(14, 0)
         stage2_matmul(14, 1)
-        group_h1(15, 0, 3, "gpsimd")
+        group_h1(15, 0, 2, "gpsimd")
         stage2_bias(14, 0)
         stage2_gelu_and_store(13, 2, 4)
         stage2_matmul(14, 2)
@@ -405,14 +419,14 @@ def tile_declayerj_pa_t_kernel(tc, h_V, h_E, W1_w, W1_b, W2_w, W2_b, out):
         stage2_bias(14, 2)
         stage2_bias(14, 3)
         stage2_gelu_and_store(14, 2, 4)
-        group_h1(15, 3, 4, "vector")
         quantise_pair(15, 0, 256)
         stage2_matmul(15, 0)
         stage2_matmul(15, 1)
+        group_h1(15, 2, 4, "vector")
         quantise_pair(15, 256, 512)
+        stage2_matmul(15, 2)
         stage2_bias(15, 0)
         stage2_gelu_and_store(15, 0, 1)
-        stage2_matmul(15, 2)
         stage2_bias(15, 1)
         stage2_gelu_and_store(15, 1, 2)
         stage2_matmul(15, 3)

from contextlib import ExitStack

import concourse.mybir as mybir
from concourse.masks import make_identity

BF16 = mybir.dt.bfloat16
F32 = mybir.dt.float32
I32 = mybir.dt.int32
U32 = mybir.dt.uint32
U8 = mybir.dt.uint8
FP8X4 = mybir.dt.float8_e4m3fn_x4
GELU = mybir.ActivationFunctionType.Gelu_apprx_tanh
ADD = mybir.AluOpType.add
MULT = mybir.AluOpType.mult

P = 128
PACK = 4
FEAT = P * PACK
NODES = 256
EDGES = 32
ROWS = NODES * EDGES
UNIT = 512
SUBS = UNIT // P
UNITS = ROWS // UNIT
BLOCK_UNITS = 8
BLOCKS = UNITS // BLOCK_UNITS

FLOPS = 2 * FEAT * FEAT * (NODES + 2 * ROWS)


def tile_declayerj_pa_t_kernel(tc, h_V, h_E, W1_w, W1_b, W2_w, W2_b, out):
    nc = tc.nc

    edge_units = h_E.rearrange("b n k c -> (b n k) c").rearrange(
        "(g p j a) c -> g j p (a c)", p=P, j=BLOCK_UNITS, a=SUBS
    )
    out_units = out.rearrange("b n k c -> (b n k) c").rearrange(
        "(g p j a) c -> g j p (a c)", p=P, j=BLOCK_UNITS, a=SUBS
    )

    with ExitStack() as ctx:
        consts = ctx.enter_context(tc.tile_pool(name="consts", bufs=1))
        prep = ctx.enter_context(tc.tile_pool(name="prep", bufs=3))
        edges_in = ctx.enter_context(tc.tile_pool(name="edges_in", bufs=UNITS))
        node_pool = ctx.enter_context(tc.tile_pool(name="node_pool", bufs=2))
        pairs = ctx.enter_context(tc.tile_pool(name="pairs", bufs=4))
        hidden = ctx.enter_context(tc.tile_pool(name="hidden", bufs=3))
        result = ctx.enter_context(tc.tile_pool(name="result", bufs=4))
        ps_t = ctx.enter_context(tc.psum_pool(name="ps_t", bufs=2))
        ps_1 = ctx.enter_context(tc.psum_pool(name="ps_1", bufs=3))
        ps_2 = ctx.enter_context(tc.psum_pool(name="ps_2", bufs=3))
        ctx.enter_context(tc.manual_schedule())

        def quantise(codes, scales, grouped):
            nc.vector.quantize_mx(out=codes.bitcast(FP8X4), scales=scales, in_=grouped)

        def mx_pass(acc, w_codes, w_scales, x_codes, x_scales, start, stop):
            nc.tensor.matmul_mx(
                out=acc,
                lhsT=w_codes.bitcast(FP8X4),
                lhsT_scale=w_scales,
                rhs=x_codes.bitcast(FP8X4),
                rhs_scale=x_scales,
                start=start,
                stop=stop,
            )

        def gpsimd_copy(dst, src):
            nc.gpsimd.tensor_scalar(out=dst, in0=src, scalar1=1.0, scalar2=0.0, op0=MULT, op1=ADD)

        def load_w1_half(half):
            raw = prep.tile([P, PACK, FEAT], BF16, name="w_raw")
            nc.sync.dma_start(
                out=raw[:].rearrange("q (u e) m -> q u (e m)", u=2),
                in_=W1_w[half * FEAT : (half + 1) * FEAT, :].rearrange("(u q e) m -> q u (e m)", u=2, e=2),
            )
            return raw

        edge_tiles = {}

        def load_unit(n):
            edge_tiles[n] = edges_in.tile([P, SUBS * FEAT], BF16, name="edge_rows")
            nc.sync.dma_start(out=edge_tiles[n][:], in_=edge_units[n // BLOCK_UNITS, n % BLOCK_UNITS])

        b1_rows = consts.tile([P, P], BF16)
        nc.vector.memset(b1_rows[:], 0.0)
        nc.scalar.dma_start(out=b1_rows[0:PACK, :], in_=W1_b.rearrange("(t p) -> t p", t=PACK))

        node_rows = consts.tile([P, 2 * FEAT], BF16)
        nc.sync.dma_start(
            out=node_rows[:].rearrange("p (a c) -> p a c", a=2),
            in_=h_V.rearrange("b n c -> (b n) c").rearrange("(a p) c -> p a c", p=P),
        )
        load_unit(0)
        w1v_raw = load_w1_half(0)
        w1e_raw = load_w1_half(1)
        load_unit(1)
        w2_raw = prep.tile([P, PACK, FEAT], BF16, name="w_raw")
        nc.sync.dma_start(
            out=w2_raw[:], in_=W2_w.rearrange("(j p) n -> p j n", j=PACK)
        )
        for n in range(2, 5):
            load_unit(n)
        b2_all = consts.tile([P, FEAT], BF16)
        nc.sync.dma_start(out=b2_all[:], in_=W2_b.partition_broadcast(P))
        for n in range(5, UNITS):
            load_unit(n)

        ident = consts.tile([P, P], F32)
        make_identity(nc, ident[:])
        warm = consts.tile([P, 2], F32)
        nc.vector.memset(warm[:], 0.0)
        nc.scalar.activation(out=warm[:, 1:2], in_=warm[:, 0:1], func=GELU)

        b1 = consts.tile([P, PACK], F32)

        def turn_b1():
            unit = consts.tile([P, PACK], BF16)
            nc.vector.tensor_copy(out=unit[:], in_=ident[:, 0:PACK])
            bank = ps_2.tile([P, FEAT], F32, name="acc2")
            nc.tensor.matmul(out=bank[:, 0:PACK], lhsT=b1_rows[:], rhs=unit[:], start=True, stop=True)
            return bank

        w1 = {}
        for half in ("nodes", "edges"):
            w1[half] = (
                prep.tile([P, FEAT * PACK], BF16, name="w_grouped", align_bytes=64),
                consts.tile([P, FEAT], U32, name="w1_codes_" + half, align_bytes=64),
                consts.tile([P, FEAT], U8, name="w1_scales_" + half, align_bytes=64),
            )

        def group_w1(half, raw, t, copy):
            copy(
                out=w1[half][0][:, t * FEAT : (t + 1) * FEAT].rearrange("q (p j) -> q p j", j=PACK),
                in_=raw[:, :, t * P : (t + 1) * P].rearrange("q j p -> q p j"),
            )

        def quantise_w1(half, t):
            grouped, codes, scales = w1[half]
            cols = slice(t * P, (t + 1) * P)
            quantise(codes[:, cols], scales[:, cols], grouped[:, t * FEAT : (t + 1) * FEAT])

        w2 = {}

        def group_w2():
            w2["grouped"] = prep.tile([P, FEAT * PACK], BF16, name="w_grouped", align_bytes=64)
            nc.vector.tensor_copy(
                out=w2["grouped"][:].rearrange("p (n j) -> p n j", j=PACK), in_=w2_raw[:].rearrange("p j n -> p n j")
            )

        def quantise_w2():
            grouped = w2["grouped"]
            w2["codes"] = consts.tile([P, FEAT], U32, name="w2_codes", align_bytes=64)
            w2["scales"] = consts.tile([P, FEAT], U8, name="w2_scales", align_bytes=64)
            quantise(w2["codes"][:], w2["scales"][:], grouped[:])

        node_codes = consts.tile([P, NODES], U32, align_bytes=64)
        node_scales = consts.tile([P, NODES], U8, align_bytes=64)
        node_grouped = consts.tile([P, NODES * PACK], BF16, align_bytes=64)

        def group_nodes():
            nc.vector.memset(node_scales[:].bitcast(I32), 0)
            node_words = node_rows[:].bitcast(F32)
            node_t = ps_t.tile([P, 2, 2, P], F32, name="words_t")
            for a in range(2):
                for u in range(2):
                    first = (2 * a + u) * P
                    nc.tensor.transpose(node_t[:, a, u, :], node_words[:, first : first + P], ident[:])
            nc.scalar.copy(
                out=node_grouped[:].bitcast(F32).rearrange("p (a r u) -> p a r u", a=2, u=2),
                in_=node_t[:].rearrange("p a u r -> p a r u"),
            )

        node_operands = {}

        def repeat_nodes(g):
            cols = slice(g * P, (g + 1) * P)
            codes = node_pool.tile([P, UNIT], U32, name="node_rep_codes", align_bytes=64)
            scales = node_pool.tile([P, UNIT], U8, name="node_rep_scales", align_bytes=64)
            nc.vector.tensor_copy(
                out=codes[:].bitcast(I32).rearrange("p (a w) -> p a w", a=SUBS),
                in_=node_codes[:, cols].bitcast(I32).unsqueeze(1).to_broadcast([P, SUBS, P]),
            )
            nc.vector.tensor_copy(
                out=scales[:].bitcast(I32).rearrange("p (a w) -> p a w", a=SUBS),
                in_=node_scales[:, cols].bitcast(I32).unsqueeze(1).to_broadcast([P, SUBS, P // 4]),
            )
            node_operands[g] = (codes, scales)

        banks_t, pair_tiles, banks_1, planes, banks_2, results = {}, {}, {}, {}, {}, {}

        def transpose_edges(n):
            words = edge_tiles[n][:].bitcast(F32)
            banks_t[n] = []
            for b in range(2):
                bank = ps_t.tile([P, 2, 2, P], F32, name="words_t")
                for a in range(2):
                    for u in range(2):
                        first = ((2 * b + a) * 2 + u) * P
                        nc.tensor.transpose(bank[:, a, u, :], words[:, first : first + P], ident[:])
                banks_t[n].append(bank)

        def pair_of(m):
            if m not in pair_tiles:
                pair_tiles[m] = (
                    pairs.tile([P, 2 * UNIT * PACK], BF16, name="pair_grouped", align_bytes=64),
                    pairs.tile([P, 2 * UNIT], U32, name="pair_codes", align_bytes=64),
                    pairs.tile([P, 2 * UNIT], U8, name="pair_scales", align_bytes=64),
                )
            return pair_tiles[m]

        def group_edges(n, b, copy=nc.vector.tensor_copy):
            grouped = pair_of(n - 3)[0][:, UNIT * PACK :]
            grouped_words = grouped.bitcast(F32).rearrange("p (a r u) -> p a r u", a=SUBS, u=2)
            copy(out=grouped_words[:, 2 * b : 2 * b + 2], in_=banks_t[n][b][:].rearrange("p a u r -> p a r u"))

        def quantise_pair(m, first, last):
            grouped, codes, scales = pair_of(m)
            quantise(codes[:, first:last], scales[:, first:last], grouped[:, first * PACK : last * PACK])

        def stage1_matmuls(n, tiles=range(PACK)):
            e_codes, e_scales = [tile[:, UNIT:] for tile in pair_of(n - 3)[1:]]
            v_codes, v_scales = node_operands[n // BLOCK_UNITS]
            w1e_codes, w1e_scales = w1["edges"][1:]
            w1v_codes, w1v_scales = w1["nodes"][1:]
            for t in tiles:
                cols = slice(t * P, (t + 1) * P)
                acc = ps_1.tile([P, UNIT], F32, name="acc1")
                mx_pass(acc[:], w1v_codes[:, cols], w1v_scales[:, cols], v_codes[:], v_scales[:], True, False)
                mx_pass(acc[:], w1e_codes[:, cols], w1e_scales[:, cols], e_codes, e_scales, False, True)
                banks_1[n, t] = acc

        def stage1_gelu(n, t):
            if t == 0:
                planes[n] = hidden.tile([P, PACK, UNIT], BF16, name="h1_planes")
            nc.scalar.activation(
                out=planes[n][:, t, :], in_=banks_1[n, t][:], func=GELU, bias=b1[:, t : t + 1], scale=1.0
            )

        def group_h1(n, first, last, engine):
            dst = pair_of(n)[0][:, first * FEAT : last * FEAT]
            src = planes[n][:, :, first * P : last * P]
            if engine == "gpsimd":
                gpsimd_copy(dst.rearrange("p (r t) -> p r t", t=PACK), src.rearrange("p t r -> p r t"))
            else:
                nc.vector.tensor_copy(
                    out=dst.rearrange("p (c i t) -> p c t i", i=4, t=PACK),
                    in_=src.rearrange("p t (c i) -> p c t i", i=4),
                )

        def stage2_matmul(n, a):
            if a == 0:
                results[n] = result.tile([P, SUBS * FEAT], F32, name="z")
            codes, scales = pair_of(n)[1:]
            cols = slice(a * P, (a + 1) * P)
            banks_2[n, a] = ps_2.tile([P, FEAT], F32, name="acc2")
            mx_pass(banks_2[n, a][:], codes[:, cols], scales[:, cols], w2["codes"][:], w2["scales"][:], True, True)

        def stage2_bias(n, a):
            nc.vector.tensor_tensor(
                out=results[n][:, a * FEAT : (a + 1) * FEAT], in0=banks_2[n, a][:], in1=b2_all[:], op=ADD
            )

        def stage2_gelu_and_store(n, first, last):
            cols = slice(first * FEAT, last * FEAT)
            nc.scalar.activation(out=results[n][:, cols], in_=results[n][:, cols], func=GELU)
            nc.sync.dma_start(out=out_units[n // BLOCK_UNITS, n % BLOCK_UNITS][:, cols], in_=results[n][:, cols])

        V_COPY, S_COPY = nc.vector.tensor_copy, nc.scalar.copy
        group_nodes()
        transpose_edges(0)
        b1_bank = turn_b1()
        quantise(node_codes[:], node_scales[:], node_grouped[:])
        repeat_nodes(0)
        group_edges(0, 0, S_COPY)
        group_edges(0, 1, S_COPY)
        group_w1("nodes", w1v_raw, 0, V_COPY)
        group_w1("nodes", w1v_raw, 1, S_COPY)
        quantise_w1("nodes", 0)
        quantise_pair(0 - 3, UNIT, 2 * UNIT)
        group_w1("edges", w1e_raw, 0, V_COPY)
        group_w1("edges", w1e_raw, 1, S_COPY)
        quantise_w1("nodes", 1)
        quantise_w1("edges", 0)
        stage1_matmuls(0, [0])
        nc.vector.tensor_copy(out=b1[:], in_=b1_bank[:, 0:PACK])
        group_w1("nodes", w1v_raw, 2, V_COPY)
        quantise_w1("edges", 1)
        stage1_matmuls(0, [1])
        group_w1("edges", w1e_raw, 2, V_COPY)
        quantise_w1("nodes", 2)
        group_w1("nodes", w1v_raw, 3, S_COPY)
        group_w1("edges", w1e_raw, 3, S_COPY)
        quantise_w1("nodes", 3)
        quantise_w1("edges", 2)
        quantise_w1("edges", 3)
        stage1_gelu(0, 0)
        stage1_gelu(0, 1)
        transpose_edges(1)
        group_edges(1, 0, S_COPY)
        group_edges(1, 1)
        stage1_matmuls(0, [2,3])
        stage1_gelu(0, 2)
        stage1_gelu(0, 3)
        quantise_pair(1 - 3, UNIT, 2 * UNIT)
        transpose_edges(2)
        group_w2()
        group_edges(2, 0, S_COPY)
        group_edges(2, 1, S_COPY)
        stage1_matmuls(1, [0])
        quantise_w2()
        quantise_pair(2 - 3, UNIT, 2 * UNIT)
        transpose_edges(3)
        repeat_nodes(1)
        stage1_matmuls(1, [1])
        stage1_gelu(1, 0)
        group_h1(0, 0, SUBS, "vector")
        group_edges(3, 0, S_COPY)
        stage1_matmuls(1, [2])
        stage1_gelu(1, 1)
        group_edges(3, 1, S_COPY)
        stage1_matmuls(1, [3])
        transpose_edges(4)
        stage1_gelu(1, 2)
        stage1_matmuls(2, [0])
        stage1_gelu(1, 3)
        quantise_pair(0, 0, 2 * UNIT)

        def in_range(n):
            return 0 <= n < UNITS

        def whole(n):
            return 0 <= n < UNITS - 1

        for i in range(2, 15):
            if in_range(i):
                stage1_matmuls(i, [1])
            if whole(i - 2):
                stage2_matmul(i - 2, 0)
            if whole(i - 2):
                stage2_matmul(i - 2, 1)
            if in_range(i):
                stage1_gelu(i, 0)
            if 1 < i < UNITS - 1:
                group_h1(i - 1, 0, SUBS, "gpsimd")
            if in_range(i + 2) and not (i < 3):
                group_edges(i + 2, 0)
            if in_range(i + 2) and (i < 3):
                group_edges(i + 2, 0, S_COPY)
            if in_range(i + 2) and not (i < 3):
                group_edges(i + 2, 1)
            if whole(i - 2):
                stage2_bias(i - 2, 0)
            if whole(i - 3):
                stage2_gelu_and_store(i - 3, 2, 4)
            if in_range(i):
                stage1_matmuls(i, [2])
            if whole(i - 2):
                stage2_matmul(i - 2, 2)
            if in_range(i):
                stage1_gelu(i, 1)
            if in_range(i + 2) and (i < 3):
                group_edges(i + 2, 1, S_COPY)
            if whole(i - 2):
                stage2_bias(i - 2, 1)
            if whole(i - 2):
                stage2_matmul(i - 2, 3)
            if in_range(i):
                stage1_matmuls(i, [3])
            if in_range(i + 3):
                transpose_edges(i + 3)
            if in_range(i):
                stage1_gelu(i, 2)
            if whole(i - 2):
                stage2_bias(i - 2, 2)
            if whole(i - 2):
                stage2_gelu_and_store(i - 2, 0, 2)
            if in_range(i + 1):
                stage1_matmuls(i + 1, [0])
            if in_range(i):
                stage1_gelu(i, 3)
            if whole(i - 2):
                stage2_bias(i - 2, 3)
            if 0 < i < UNITS and i != 13:
                quantise_pair(i - 1, 0, 2 * UNIT if in_range(i + 2) else UNIT)
            if i == 13:
                quantise_pair(i - 1, 0, UNIT)
                quantise_pair(i - 1, UNIT, 2 * UNIT)

        stage1_matmuls(15, [1])
        stage2_matmul(13, 0)
        stage2_matmul(13, 1)
        stage1_gelu(15, 0)
        group_h1(14, 0, 2, "vector")
        group_h1(14, 2, 4, "gpsimd")
        stage2_bias(13, 0)
        stage2_bias(13, 1)
        stage2_gelu_and_store(12, 2, 4)
        stage1_matmuls(15, [2])
        stage2_matmul(13, 2)
        stage1_gelu(15, 1)
        stage1_matmuls(15, [3])
        stage2_matmul(13, 3)
        stage1_gelu(15, 2)
        stage2_bias(13, 2)
        quantise_pair(14, 0, 512)
        stage2_gelu_and_store(13, 0, 2)
        stage2_bias(13, 3)
        stage1_gelu(15, 3)
        stage2_matmul(14, 0)
        stage2_matmul(14, 1)
        group_h1(15, 0, 2, "gpsimd")
        stage2_bias(14, 0)
        stage2_gelu_and_store(13, 2, 4)
        stage2_matmul(14, 2)
        stage2_bias(14, 1)
        stage2_gelu_and_store(14, 0, 2)
        stage2_matmul(14, 3)
        stage2_bias(14, 2)
        stage2_bias(14, 3)
        stage2_gelu_and_store(14, 2, 4)
        quantise_pair(15, 0, 256)
        stage2_matmul(15, 0)
        stage2_matmul(15, 1)
        group_h1(15, 2, 4, "vector")
        quantise_pair(15, 256, 512)
        stage2_matmul(15, 2)
        stage2_bias(15, 0)
        stage2_gelu_and_store(15, 0, 1)
        stage2_bias(15, 1)
        stage2_gelu_and_store(15, 1, 2)
        stage2_matmul(15, 3)
        stage2_bias(15, 2)
        stage2_gelu_and_store(15, 2, 3)
        stage2_bias(15, 3)
        stage2_gelu_and_store(15, 3, 4)
